import numpy as np
import ml_dtypes


def mxq(x, axis, fmt="e4m3"):
    dtype, down = {"e4m3": (ml_dtypes.float8_e4m3fn, 7), "e5m2": (ml_dtypes.float8_e5m2, 14)}[fmt]
    v = np.moveaxis(np.asarray(x, np.float32).astype(ml_dtypes.bfloat16).astype(np.float64), axis, -1)
    blocks = v.reshape(v.shape[:-1] + (-1, 32))
    amax = np.abs(blocks).max(-1, keepdims=True)
    byte = np.maximum(np.where(amax > 0, np.frexp(amax)[1] - 1 + 127, 0) - down, 1)
    scale = np.exp2(byte - 127.0)
    codes = (blocks / scale).astype(np.float32).astype(dtype).astype(np.float64)
    return np.moveaxis((codes * scale).reshape(v.shape), -1, axis)


WIDE = False


def mx_kscale(k):
    if not WIDE:
        return np.ones(k)
    levels = np.array([10, -10, 5, -5, 0])
    a = np.random.permutation(np.resize(levels, k // 512 * 4)).reshape(k // 512, 4)
    idx = np.arange(k)
    return np.exp2(a[idx // 512, idx % 128 // 32])


BF16 = ml_dtypes.bfloat16


def bf(x):
    return np.asarray(x, np.float32).astype(BF16)


def f64(x):
    return np.asarray(x).astype(np.float64)


E2M1 = np.array([0.0, 0.5, 1.0, 1.5, 2.0, 3.0, 4.0, 6.0, -0.0, -0.5, -1.0, -1.5, -2.0, -3.0, -4.0, -6.0])


def pack_weight(w, fmt):
    k, n = w.shape
    w = f64(bf(w)).reshape(k // 32, 32, n)
    amax = np.abs(w).max(1)
    if fmt == "e4m3":
        byte = np.frexp(amax)[1] - 1 + 127 - 7
    else:
        mant, ex = np.frexp(amax / 6.0)
        byte = np.where(mant > 0.5, ex, ex - 1) + 127
    byte = np.clip(np.where(amax > 0, byte, 1), 1, 254)
    scaled = (w * np.exp2(127.0 - byte)[:, None, :]).reshape(k, n).astype(np.float32)
    by_word = np.ascontiguousarray(scaled.reshape(k // 512, 128, 4, n).transpose(0, 1, 3, 2))
    if fmt == "e4m3":
        words = by_word.astype(ml_dtypes.float8_e4m3fn).view(np.uint8)
    else:
        c = by_word.astype(ml_dtypes.float4_e2m1fn).view(np.uint8) & 0xF
        words = c[..., 0::2] | (c[..., 1::2] << 4)
    return np.ascontiguousarray(words), np.ascontiguousarray(byte.astype(np.uint8).reshape(k // 512, 16, n))


def unpack_weight(words, scales, fmt):
    g, p, n, _ = words.shape
    if fmt == "e4m3":
        vals = np.ascontiguousarray(words).view(ml_dtypes.float8_e4m3fn).astype(np.float64)
    else:
        nib = np.empty((g, p, n, 4), np.uint8)
        nib[..., 0::2] = words & 0xF
        nib[..., 1::2] = words >> 4
        vals = E2M1[nib]
    vals = vals * np.repeat(np.exp2(scales.astype(np.float64) - 127.0), 8, axis=1)[..., None]
    return vals.transpose(0, 1, 3, 2).reshape(g * 512, n)


P, N, Z, H1, H2, C = 8, 256, 16, 512, 2048, 256
EPS = 1e-5


def batch_norm(h, gamma, beta):
    mu = h.mean(axis=1, keepdims=True)
    var = h.var(axis=1, keepdims=True)
    return (h - mu) * (1.0 / np.sqrt(var + EPS)) * gamma[:, None, :] + beta[:, None, :]


def setup_inputs():
    r = np.random.standard_normal
    t = mx_kscale(H2)
    sd = np.where(np.random.random((P, 1, H2)) < 0.25, np.sqrt(EPS), 1.0)
    h7_pre = bf((r((P, N, H2)) + 0.5 * r((P, 1, H2))) * sd)
    g7 = bf((1.0 + 0.1 * r((P, H2))) * t)
    be7 = bf(0.3 * r((P, H2)) * t)
    w8 = 1.5 * r((P, C, H2)) / np.sqrt(H2) / t
    cat = np.ascontiguousarray(w8.swapaxes(1, 2)).reshape(-1, C)
    words, scales = pack_weight(cat, "e4m3")
    b8 = bf(0.5 * r((P, C)))
    return {"h7_pre": h7_pre,
            "g7": g7,
            "be7": be7,
            "W8_words": words,
            "W8_scales": scales,
            "b8": b8}


def reference(h7_pre, g7, be7, W8_words, W8_scales, b8):
    a = np.maximum(batch_norm(f64(h7_pre), f64(g7), f64(be7)), 0.0)
    y = (mxq(a, 2, "e4m3") @ unpack_weight(W8_words, W8_scales, "e4m3").reshape(P, H2, C)) + f64(b8)[:, None, :]
    em = 1.0 / (1.0 + np.exp(-y))
    return em.transpose(1, 0, 2)

@@ -1,0 +1,244 @@
+from contextlib import ExitStack
+
+import concourse.mybir as mybir
+from concourse.masks import make_identity
+
+F32 = mybir.dt.float32
+BF16 = mybir.dt.bfloat16
+I32 = mybir.dt.int32
+U32 = mybir.dt.uint32
+U8 = mybir.dt.uint8
+FP8X4 = mybir.dt.float8_e4m3fn_x4
+ALU = mybir.AluOpType
+ACT = mybir.ActivationFunctionType
+
+P = 128
+BLOCKS = 8
+ROWS = 256
+ROW_TILES = ROWS // P
+FEATURES = 2048
+CHANNELS = 256
+PACK = 4
+K_PASS = P * PACK
+PASSES = FEATURES // K_PASS
+GROUPS = BLOCKS * PASSES
+PAIR = 2
+HALF = 2
+EPS = 1e-5
+LEAD = 4
+
+FLOPS = 2 * BLOCKS * ROWS * FEATURES * CHANNELS
+
+
+def tile_decoder_pb_e_kernel(tc, h7_pre, g7, be7, W8_words, W8_scales, b8, out):
+    nc = tc.nc
+    with ExitStack() as ctx:
+        keep = ctx.enter_context(tc.tile_pool(name="keep", bufs=1))
+        small = ctx.enter_context(tc.tile_pool(name="small", bufs=4))
+        work = ctx.enter_context(tc.tile_pool(name="work", bufs=3))
+        psum_stats = ctx.enter_context(tc.psum_pool(name="psum_stats", bufs=2))
+        psum_norm = ctx.enter_context(tc.psum_pool(name="psum_norm", bufs=4))
+        psum_out = ctx.enter_context(tc.psum_pool(name="psum_out", bufs=2))
+        ctx.enter_context(tc.manual_schedule())
+
+        w_planes = keep.tile([P, GROUPS, CHANNELS], U8, align_bytes=64)
+        nc.vector.memset(w_planes[:].bitcast(I32), 0)
+        gain_rows = keep.tile([P, K_PASS], BF16)
+        nc.vector.memset(gain_rows[2 * GROUPS : P, :], 0.0)
+        minus_half = keep.tile([P, HALF * PACK], F32)
+        nc.vector.memset(minus_half[:], -0.5)
+        ident = keep.tile([P, P], F32)
+        make_identity(nc, ident[:])
+
+        x_rows = {}
+        w_words = {}
+
+        def load_x(b):
+            for r in range(ROW_TILES):
+                x_tile = keep.tile([P, FEATURES], BF16, name="x_%d_%d" % (b, r))
+                nc.sync.dma_start(out=x_tile[:], in_=h7_pre[b, r * P : (r + 1) * P, :])
+                x_rows[(b, r)] = x_tile
+
+        def load_w(b):
+            w_tile = keep.tile([P, PASSES, CHANNELS], U32, name="w_words_%d" % b, align_bytes=64)
+            nc.sync.dma_start(
+                out=w_tile[:].bitcast(I32),
+                in_=W8_words[PASSES * b : PASSES * (b + 1)].rearrange("g p n t -> p g (n t)").bitcast(I32),
+            )
+            w_words[b] = w_tile
+
+        nc.scalar.dma_start(out=gain_rows[0:GROUPS, :], in_=g7.rearrange("b (g k) -> (b g) k", g=PASSES))
+        nc.scalar.dma_start(out=gain_rows[GROUPS : 2 * GROUPS, :], in_=be7.rearrange("b (g k) -> (b g) k", g=PASSES))
+        bias_all = keep.tile([P, BLOCKS, CHANNELS], BF16)
+        nc.scalar.dma_start(
+            out=bias_all[:].rearrange("p b c -> p (b c)"),
+            in_=b8.rearrange("b c -> (b c)").partition_broadcast(P),
+        )
+
+        load_x(0)
+        load_x(1)
+        load_w(0)
+        scale_rows = W8_scales.rearrange("g (q r) c -> r q g c", r=4)
+        for r in range(4):
+            nc.sync.dma_start(out=w_planes[r:P:32, :, :].bitcast(I32), in_=scale_rows[r].bitcast(I32))
+        for b in range(2, BLOCKS):
+            load_x(b)
+            load_w(b - 1)
+        load_w(BLOCKS - 1)
+
+        def transpose_group(bank, b, g):
+            for r in range(ROW_TILES):
+                words = x_rows[(b, r)][:].bitcast(F32)
+                for u in range(PAIR):
+                    nc.tensor.transpose(
+                        bank[:, u, r * P : (r + 1) * P],
+                        words[:, (K_PASS // PAIR) * g + u : (K_PASS // PAIR) * (g + 1) : PAIR],
+                        ident[:],
+                    )
+
+        gain_bank = psum_stats.tile([P, PAIR, P], F32, tag="stat_bank")
+        for u in range(PAIR):
+            nc.tensor.transpose(gain_bank[:, u, :], gain_rows[:].bitcast(F32)[:, u : K_PASS // PAIR : PAIR], ident[:])
+        gain_cols = keep.tile([P, 2 * GROUPS, PAIR, PAIR], F32)
+        nc.vector.tensor_copy(
+            out=gain_cols[:],
+            in_=gain_bank[:].bitcast(BF16).rearrange("p u (r e) -> p r u e", e=PAIR)[:, 0 : 2 * GROUPS],
+        )
+
+        moments = {}
+        affine = {}
+        norm_banks = {}
+        planes_of = {}
+        quantised = {}
+        sums = {}
+        logits_of = {}
+
+        def statistics(group):
+            b, g = divmod(group, PASSES)
+            half, place = divmod(group, HALF)
+            if place == 0:
+                moments_tile = small.tile([P, HALF * PAIR * 6], F32, name="moments")
+                moments[half] = moments_tile
+            stat_bank = psum_stats.tile([P, PAIR, ROWS], F32, tag="stat_bank")
+            transpose_group(stat_bank, b, g)
+            for u in range(PAIR):
+                at = 6 * (PAIR * place + u)
+                nc.vector.bn_stats(out=moments[half][:, at : at + 6], in_=stat_bank[:, u, :].bitcast(BF16))
+            if place == HALF - 1:
+                scale_and_shift(half)
+
+        def scale_and_shift(half):
+            triples = moments[half][:].rearrange("p (f s) -> p f s", s=3)
+            width = HALF * PACK
+            gain = gain_cols[:, HALF * half : HALF * (half + 1)].rearrange("p r u e -> p (r u e)")
+            beta = gain_cols[:, GROUPS + HALF * half : GROUPS + HALF * (half + 1)].rearrange("p r u e -> p (r u e)")
+            var_eps = small.tile([P, width], F32)
+            nc.gpsimd.tensor_scalar(
+                out=var_eps[:], in0=triples[:, :, 2], scalar1=1.0 / ROWS, scalar2=EPS, op0=ALU.mult, op1=ALU.add
+            )
+            rstd = small.tile([P, width], F32)
+            nc.gpsimd.tensor_tensor(out=rstd[:], in0=var_eps[:], in1=minus_half[:], op=ALU.pow)
+            scale = small.tile([P, width], F32)
+            nc.gpsimd.tensor_tensor(out=scale[:], in0=rstd[:], in1=gain, op=ALU.mult)
+            mean_scaled = small.tile([P, width], F32)
+            nc.gpsimd.tensor_tensor(out=mean_scaled[:], in0=triples[:, :, 1], in1=scale[:], op=ALU.mult)
+            shift = small.tile([P, width], F32)
+            nc.gpsimd.tensor_tensor(out=shift[:], in0=beta, in1=mean_scaled[:], op=ALU.subtract)
+            affine[half] = (scale, shift)
+
+        def fill_norm_bank(group):
+            b, g = divmod(group, PASSES)
+            norm_bank = psum_norm.tile([P, PAIR, ROWS], F32)
+            transpose_group(norm_bank, b, g)
+            norm_banks[group] = norm_bank
+
+        def normalise(group):
+            half, place = divmod(group, HALF)
+            scale, shift = affine[half]
+            planes = work.tile([P, PACK, ROWS], BF16, bufs=4)
+            for u in range(PAIR):
+                pairs = norm_banks[group][:, u, :].bitcast(BF16).rearrange("p (n e) -> p n e", e=PAIR)
+                for e in range(PAIR):
+                    t = PAIR * u + e
+                    f = PACK * place + t
+                    nc.scalar.activation(
+                        out=planes[:, t, :],
+                        in_=pairs[:, :, e],
+                        func=ACT.Relu,
+                        bias=shift[:, f : f + 1],
+                        scale=scale[:, f : f + 1],
+                    )
+            planes_of[group] = planes
+
+        def regroup(group):
+            b, g = divmod(group, PASSES)
+            if g == 0:
+                grouped = work.tile([P, PASSES, ROWS, PACK], BF16, align_bytes=64)
+                a_codes = work.tile([P, PASSES, ROWS], U32, align_bytes=64)
+                a_planes = work.tile([P, PASSES, ROWS], U8, align_bytes=64)
+                quantised[b] = (grouped, a_codes, a_planes)
+            side_by_side = quantised[b][0][:, g].rearrange("p (c i) t -> p c t i", i=4)
+            by_feature = planes_of[group][:].rearrange("p t (c i) -> p c t i", i=4)
+            if group % 2 == 0:
+                nc.vector.tensor_copy(out=side_by_side, in_=by_feature)
+            else:
+                nc.scalar.copy(out=side_by_side, in_=by_feature)
+
+        def quantise(group):
+            b, g = divmod(group, PASSES)
+            grouped, a_codes, a_planes = quantised[b]
+            nc.vector.quantize_mx(
+                out=a_codes[:, g, :].bitcast(FP8X4),
+                scales=a_planes[:, g, :],
+                in_=grouped[:, g].rearrange("p n t -> p (n t)"),
+            )
+
+        def multiply(b):
+            grouped, a_codes, a_planes = quantised[b]
+            acc = psum_out.tile([P, ROW_TILES, CHANNELS], F32)
+            for r in range(ROW_TILES):
+                rows = slice(r * P, (r + 1) * P)
+                for g in range(PASSES):
+                    nc.tensor.matmul_mx(
+                        out=acc[:, r, :],
+                        lhsT=a_codes[:, g, rows].bitcast(FP8X4),
+                        lhsT_scale=a_planes[:, g, rows],
+                        rhs=w_words[b][:, g, :].bitcast(FP8X4),
+                        rhs_scale=w_planes[:, PASSES * b + g, :],
+                        start=(g == 0),
+                        stop=(g == PASSES - 1),
+                    )
+            sums[b] = acc
+
+        def add_bias(b):
+            logits = work.tile([P, ROW_TILES, CHANNELS], F32)
+            nc.vector.tensor_tensor(
+                out=logits[:],
+                in0=sums[b][:],
+                in1=bias_all[:, b, :].unsqueeze(1).to_broadcast([P, ROW_TILES, CHANNELS]),
+                op=ALU.add,
+            )
+            logits_of[b] = logits
+
+        def squash_and_store(b):
+            probs = work.tile([P, ROW_TILES, CHANNELS], F32)
+            nc.scalar.activation(out=probs[:], in_=logits_of[b][:], func=ACT.Sigmoid)
+            nc.scalar.dma_start(out=out.rearrange("(r n) b c -> n r b c", r=ROW_TILES)[:, :, b, :], in_=probs[:])
+
+        def for_group(stage, group):
+            if 0 <= group < GROUPS:
+                stage(group)
+
+        def for_block(stage, last_group):
+            if 0 <= last_group < GROUPS and last_group % PASSES == PASSES - 1:
+                stage(last_group // PASSES)
+
+        for step in range(-LEAD, GROUPS + 6):
+            for_group(statistics, step + LEAD)
+            for_group(fill_norm_bank, step + 1)
+            for_group(normalise, step)
+            for_group(regroup, step - 1)
+            for_group(quantise, step - 2)
+            for_block(multiply, step - 3)
+            for_block(add_bias, step - 4)
+            for_block(squash_and_store, step - 5)

@@ -25,7 +25,7 @@ GROUPS = BLOCKS * PASSES
 PAIR = 2
 HALF = 2
 EPS = 1e-5
-LEAD = 4
+LEAD = 6
 
 FLOPS = 2 * BLOCKS * ROWS * FEATURES * CHANNELS
 
@@ -34,7 +34,7 @@ def tile_decoder_pb_e_kernel(tc, h7_pre, g7, be7, W8_words, W8_scales, b8, out):
     nc = tc.nc
     with ExitStack() as ctx:
         keep = ctx.enter_context(tc.tile_pool(name="keep", bufs=1))
-        small = ctx.enter_context(tc.tile_pool(name="small", bufs=4))
+        small = ctx.enter_context(tc.tile_pool(name="small", bufs=6))
         work = ctx.enter_context(tc.tile_pool(name="work", bufs=3))
         psum_stats = ctx.enter_context(tc.psum_pool(name="psum_stats", bufs=2))
         psum_norm = ctx.enter_context(tc.psum_pool(name="psum_norm", bufs=4))
@@ -56,8 +56,11 @@ def tile_decoder_pb_e_kernel(tc, h7_pre, g7, be7, W8_words, W8_scales, b8, out):
         def load_x(b):
             for r in range(ROW_TILES):
                 x_tile = keep.tile([P, FEATURES], BF16, name="x_%d_%d" % (b, r))
-                nc.sync.dma_start(out=x_tile[:], in_=h7_pre[b, r * P : (r + 1) * P, :])
                 x_rows[(b, r)] = x_tile
+            for first in range(0, FEATURES, HALF * K_PASS):
+                cols = slice(first, first + HALF * K_PASS)
+                for r in range(ROW_TILES):
+                    nc.sync.dma_start(out=x_rows[(b, r)][:, cols], in_=h7_pre[b, r * P : (r + 1) * P, cols])
 
         def load_w(b):
             w_tile = keep.tile([P, PASSES, CHANNELS], U32, name="w_words_%d" % b, align_bytes=64)
@@ -69,11 +72,6 @@ def tile_decoder_pb_e_kernel(tc, h7_pre, g7, be7, W8_words, W8_scales, b8, out):
 
         nc.scalar.dma_start(out=gain_rows[0:GROUPS, :], in_=g7.rearrange("b (g k) -> (b g) k", g=PASSES))
         nc.scalar.dma_start(out=gain_rows[GROUPS : 2 * GROUPS, :], in_=be7.rearrange("b (g k) -> (b g) k", g=PASSES))
-        bias_all = keep.tile([P, BLOCKS, CHANNELS], BF16)
-        nc.scalar.dma_start(
-            out=bias_all[:].rearrange("p b c -> p (b c)"),
-            in_=b8.rearrange("b c -> (b c)").partition_broadcast(P),
-        )
 
         load_x(0)
         load_x(1)
@@ -81,6 +79,11 @@ def tile_decoder_pb_e_kernel(tc, h7_pre, g7, be7, W8_words, W8_scales, b8, out):
         scale_rows = W8_scales.rearrange("g (q r) c -> r q g c", r=4)
         for r in range(4):
             nc.sync.dma_start(out=w_planes[r:P:32, :, :].bitcast(I32), in_=scale_rows[r].bitcast(I32))
+        bias_all = keep.tile([P, BLOCKS, CHANNELS], BF16)
+        nc.sync.dma_start(
+            out=bias_all[:].rearrange("p b c -> p (b c)"),
+            in_=b8.rearrange("b c -> (b c)").partition_broadcast(P),
+        )
         for b in range(2, BLOCKS):
             load_x(b)
             load_w(b - 1)
@@ -106,6 +109,7 @@ def tile_decoder_pb_e_kernel(tc, h7_pre, g7, be7, W8_words, W8_scales, b8, out):
         )
 
         moments = {}
+        rstd_of = {}
         affine = {}
         norm_banks = {}
         planes_of = {}
@@ -124,26 +128,27 @@ def tile_decoder_pb_e_kernel(tc, h7_pre, g7, be7, W8_words, W8_scales, b8, out):
             for u in range(PAIR):
                 at = 6 * (PAIR * place + u)
                 nc.vector.bn_stats(out=moments[half][:, at : at + 6], in_=stat_bank[:, u, :].bitcast(BF16))
-            if place == HALF - 1:
-                scale_and_shift(half)
 
-        def scale_and_shift(half):
+        def inverse_deviation(half):
             triples = moments[half][:].rearrange("p (f s) -> p f s", s=3)
-            width = HALF * PACK
-            gain = gain_cols[:, HALF * half : HALF * (half + 1)].rearrange("p r u e -> p (r u e)")
-            beta = gain_cols[:, GROUPS + HALF * half : GROUPS + HALF * (half + 1)].rearrange("p r u e -> p (r u e)")
-            var_eps = small.tile([P, width], F32)
+            var_eps = small.tile([P, HALF * PACK], F32)
             nc.gpsimd.tensor_scalar(
                 out=var_eps[:], in0=triples[:, :, 2], scalar1=1.0 / ROWS, scalar2=EPS, op0=ALU.mult, op1=ALU.add
             )
-            rstd = small.tile([P, width], F32)
+            rstd = small.tile([P, HALF * PACK], F32)
             nc.gpsimd.tensor_tensor(out=rstd[:], in0=var_eps[:], in1=minus_half[:], op=ALU.pow)
-            scale = small.tile([P, width], F32)
-            nc.gpsimd.tensor_tensor(out=scale[:], in0=rstd[:], in1=gain, op=ALU.mult)
-            mean_scaled = small.tile([P, width], F32)
-            nc.gpsimd.tensor_tensor(out=mean_scaled[:], in0=triples[:, :, 1], in1=scale[:], op=ALU.mult)
-            shift = small.tile([P, width], F32)
-            nc.gpsimd.tensor_tensor(out=shift[:], in0=beta, in1=mean_scaled[:], op=ALU.subtract)
+            rstd_of[half] = rstd
+
+        def scale_and_shift(half):
+            triples = moments[half][:].rearrange("p (f s) -> p f s", s=3)
+            gain = gain_cols[:, HALF * half : HALF * (half + 1)].rearrange("p r u e -> p (r u e)")
+            beta = gain_cols[:, GROUPS + HALF * half : GROUPS + HALF * (half + 1)].rearrange("p r u e -> p (r u e)")
+            scale = small.tile([P, HALF * PACK], F32)
+            nc.vector.tensor_tensor(out=scale[:], in0=rstd_of[half][:], in1=gain, op=ALU.mult)
+            mean_scaled = small.tile([P, HALF * PACK], F32)
+            nc.vector.tensor_tensor(out=mean_scaled[:], in0=triples[:, :, 1], in1=scale[:], op=ALU.mult)
+            shift = small.tile([P, HALF * PACK], F32)
+            nc.vector.tensor_tensor(out=shift[:], in0=beta, in1=mean_scaled[:], op=ALU.subtract)
             affine[half] = (scale, shift)
 
         def fill_norm_bank(group):
@@ -155,7 +160,7 @@ def tile_decoder_pb_e_kernel(tc, h7_pre, g7, be7, W8_words, W8_scales, b8, out):
         def normalise(group):
             half, place = divmod(group, HALF)
             scale, shift = affine[half]
-            planes = work.tile([P, PACK, ROWS], BF16, bufs=4)
+            planes = work.tile([P, PACK, ROWS], BF16, bufs=6)
             for u in range(PAIR):
                 pairs = norm_banks[group][:, u, :].bitcast(BF16).rearrange("p (n e) -> p n e", e=PAIR)
                 for e in range(PAIR):
@@ -179,7 +184,7 @@ def tile_decoder_pb_e_kernel(tc, h7_pre, g7, be7, W8_words, W8_scales, b8, out):
                 quantised[b] = (grouped, a_codes, a_planes)
             side_by_side = quantised[b][0][:, g].rearrange("p (c i) t -> p c t i", i=4)
             by_feature = planes_of[group][:].rearrange("p t (c i) -> p c t i", i=4)
-            if group % 2 == 0:
+            if group % 2 == 1:
                 nc.vector.tensor_copy(out=side_by_side, in_=by_feature)
             else:
                 nc.scalar.copy(out=side_by_side, in_=by_feature)
@@ -229,16 +234,22 @@ def tile_decoder_pb_e_kernel(tc, h7_pre, g7, be7, W8_words, W8_scales, b8, out):
             if 0 <= group < GROUPS:
                 stage(group)
 
+        def for_half(stage, last_group):
+            if 0 <= last_group < GROUPS and last_group % HALF == HALF - 1:
+                stage(last_group // HALF)
+
         def for_block(stage, last_group):
             if 0 <= last_group < GROUPS and last_group % PASSES == PASSES - 1:
                 stage(last_group // PASSES)
 
-        for step in range(-LEAD, GROUPS + 6):
+        for step in range(-LEAD, GROUPS + 7):
             for_group(statistics, step + LEAD)
+            for_half(inverse_deviation, step + LEAD)
+            for_half(scale_and_shift, step + LEAD - 2)
             for_group(fill_norm_bank, step + 1)
             for_group(normalise, step)
             for_group(regroup, step - 1)
-            for_group(quantise, step - 2)
-            for_block(multiply, step - 3)
-            for_block(add_bias, step - 4)
-            for_block(squash_and_store, step - 5)
+            for_group(quantise, step - 3)
+            for_block(multiply, step - 4)
+            for_block(add_bias, step - 5)
+            for_block(squash_and_store, step - 6)

@@ -25,7 +25,7 @@ GROUPS = BLOCKS * PASSES
 PAIR = 2
 HALF = 2
 EPS = 1e-5
-LEAD = 6
+LEAD = 8
 
 FLOPS = 2 * BLOCKS * ROWS * FEATURES * CHANNELS
 
@@ -34,7 +34,7 @@ def tile_decoder_pb_e_kernel(tc, h7_pre, g7, be7, W8_words, W8_scales, b8, out):
     nc = tc.nc
     with ExitStack() as ctx:
         keep = ctx.enter_context(tc.tile_pool(name="keep", bufs=1))
-        small = ctx.enter_context(tc.tile_pool(name="small", bufs=6))
+        small = ctx.enter_context(tc.tile_pool(name="small", bufs=8))
         work = ctx.enter_context(tc.tile_pool(name="work", bufs=3))
         psum_stats = ctx.enter_context(tc.psum_pool(name="psum_stats", bufs=2))
         psum_norm = ctx.enter_context(tc.psum_pool(name="psum_norm", bufs=4))
@@ -72,6 +72,8 @@ def tile_decoder_pb_e_kernel(tc, h7_pre, g7, be7, W8_words, W8_scales, b8, out):
 
         nc.scalar.dma_start(out=gain_rows[0:GROUPS, :], in_=g7.rearrange("b (g k) -> (b g) k", g=PASSES))
         nc.scalar.dma_start(out=gain_rows[GROUPS : 2 * GROUPS, :], in_=be7.rearrange("b (g k) -> (b g) k", g=PASSES))
+        warm = keep.tile([P, 1], F32)
+        nc.scalar.activation(out=warm[:], in_=minus_half[:, 0:1], func=ACT.Sigmoid)
 
         load_x(0)
         load_x(1)
@@ -144,11 +146,11 @@ def tile_decoder_pb_e_kernel(tc, h7_pre, g7, be7, W8_words, W8_scales, b8, out):
             gain = gain_cols[:, HALF * half : HALF * (half + 1)].rearrange("p r u e -> p (r u e)")
             beta = gain_cols[:, GROUPS + HALF * half : GROUPS + HALF * (half + 1)].rearrange("p r u e -> p (r u e)")
             scale = small.tile([P, HALF * PACK], F32)
-            nc.vector.tensor_tensor(out=scale[:], in0=rstd_of[half][:], in1=gain, op=ALU.mult)
+            nc.gpsimd.tensor_tensor(out=scale[:], in0=rstd_of[half][:], in1=gain, op=ALU.mult)
             mean_scaled = small.tile([P, HALF * PACK], F32)
-            nc.vector.tensor_tensor(out=mean_scaled[:], in0=triples[:, :, 1], in1=scale[:], op=ALU.mult)
+            nc.gpsimd.tensor_tensor(out=mean_scaled[:], in0=triples[:, :, 1], in1=scale[:], op=ALU.mult)
             shift = small.tile([P, HALF * PACK], F32)
-            nc.vector.tensor_tensor(out=shift[:], in0=beta, in1=mean_scaled[:], op=ALU.subtract)
+            nc.gpsimd.tensor_tensor(out=shift[:], in0=beta, in1=mean_scaled[:], op=ALU.subtract)
             affine[half] = (scale, shift)
 
         def fill_norm_bank(group):
@@ -184,10 +186,10 @@ def tile_decoder_pb_e_kernel(tc, h7_pre, g7, be7, W8_words, W8_scales, b8, out):
                 quantised[b] = (grouped, a_codes, a_planes)
             side_by_side = quantised[b][0][:, g].rearrange("p (c i) t -> p c t i", i=4)
             by_feature = planes_of[group][:].rearrange("p t (c i) -> p c t i", i=4)
-            if group % 2 == 1:
-                nc.vector.tensor_copy(out=side_by_side, in_=by_feature)
-            else:
+            if g == 0:
                 nc.scalar.copy(out=side_by_side, in_=by_feature)
+            else:
+                nc.vector.tensor_copy(out=side_by_side, in_=by_feature)
 
         def quantise(group):
             b, g = divmod(group, PASSES)
@@ -226,9 +228,9 @@ def tile_decoder_pb_e_kernel(tc, h7_pre, g7, be7, W8_words, W8_scales, b8, out):
             logits_of[b] = logits
 
         def squash_and_store(b):
-            probs = work.tile([P, ROW_TILES, CHANNELS], F32)
+            probs = work.tile([P, ROW_TILES, CHANNELS], F32, bufs=BLOCKS)
             nc.scalar.activation(out=probs[:], in_=logits_of[b][:], func=ACT.Sigmoid)
-            nc.scalar.dma_start(out=out.rearrange("(r n) b c -> n r b c", r=ROW_TILES)[:, :, b, :], in_=probs[:])
+            nc.sync.dma_start(out=out.rearrange("(r n) b c -> n r b c", r=ROW_TILES)[:, :, b, :], in_=probs[:])
 
         def for_group(stage, group):
             if 0 <= group < GROUPS:
@@ -245,7 +247,7 @@ def tile_decoder_pb_e_kernel(tc, h7_pre, g7, be7, W8_words, W8_scales, b8, out):
         for step in range(-LEAD, GROUPS + 7):
             for_group(statistics, step + LEAD)
             for_half(inverse_deviation, step + LEAD)
-            for_half(scale_and_shift, step + LEAD - 2)
+            for_half(scale_and_shift, step + LEAD)
             for_group(fill_norm_bank, step + 1)
             for_group(normalise, step)
             for_group(regroup, step - 1)

@@ -111,8 +111,9 @@ def tile_decoder_pb_e_kernel(tc, h7_pre, g7, be7, W8_words, W8_scales, b8, out):
         )
 
         moments = {}
-        rstd_of = {}
-        affine = {}
+        scale_of = {}
+        mean_scaled_of = {}
+        shift_of = {}
         norm_banks = {}
         planes_of = {}
         quantised = {}
@@ -131,7 +132,7 @@ def tile_decoder_pb_e_kernel(tc, h7_pre, g7, be7, W8_words, W8_scales, b8, out):
                 at = 6 * (PAIR * place + u)
                 nc.vector.bn_stats(out=moments[half][:, at : at + 6], in_=stat_bank[:, u, :].bitcast(BF16))
 
-        def inverse_deviation(half):
+        def scale_from_variance(half):
             triples = moments[half][:].rearrange("p (f s) -> p f s", s=3)
             var_eps = small.tile([P, HALF * PACK], F32)
             nc.gpsimd.tensor_scalar(
@@ -139,19 +140,22 @@ def tile_decoder_pb_e_kernel(tc, h7_pre, g7, be7, W8_words, W8_scales, b8, out):
             )
             rstd = small.tile([P, HALF * PACK], F32)
             nc.gpsimd.tensor_tensor(out=rstd[:], in0=var_eps[:], in1=minus_half[:], op=ALU.pow)
-            rstd_of[half] = rstd
-
-        def scale_and_shift(half):
-            triples = moments[half][:].rearrange("p (f s) -> p f s", s=3)
             gain = gain_cols[:, HALF * half : HALF * (half + 1)].rearrange("p r u e -> p (r u e)")
-            beta = gain_cols[:, GROUPS + HALF * half : GROUPS + HALF * (half + 1)].rearrange("p r u e -> p (r u e)")
             scale = small.tile([P, HALF * PACK], F32)
-            nc.gpsimd.tensor_tensor(out=scale[:], in0=rstd_of[half][:], in1=gain, op=ALU.mult)
+            nc.gpsimd.tensor_tensor(out=scale[:], in0=rstd[:], in1=gain, op=ALU.mult)
+            scale_of[half] = scale
+
+        def scaled_mean(half):
+            triples = moments[half][:].rearrange("p (f s) -> p f s", s=3)
             mean_scaled = small.tile([P, HALF * PACK], F32)
-            nc.gpsimd.tensor_tensor(out=mean_scaled[:], in0=triples[:, :, 1], in1=scale[:], op=ALU.mult)
+            nc.vector.tensor_tensor(out=mean_scaled[:], in0=triples[:, :, 1], in1=scale_of[half][:], op=ALU.mult)
+            mean_scaled_of[half] = mean_scaled
+
+        def shift_from_mean(half):
+            beta = gain_cols[:, GROUPS + HALF * half : GROUPS + HALF * (half + 1)].rearrange("p r u e -> p (r u e)")
             shift = small.tile([P, HALF * PACK], F32)
-            nc.gpsimd.tensor_tensor(out=shift[:], in0=beta, in1=mean_scaled[:], op=ALU.subtract)
-            affine[half] = (scale, shift)
+            nc.vector.tensor_tensor(out=shift[:], in0=beta, in1=mean_scaled_of[half][:], op=ALU.subtract)
+            shift_of[half] = shift
 
         def fill_norm_bank(group):
             b, g = divmod(group, PASSES)
@@ -161,7 +165,7 @@ def tile_decoder_pb_e_kernel(tc, h7_pre, g7, be7, W8_words, W8_scales, b8, out):
 
         def normalise(group):
             half, place = divmod(group, HALF)
-            scale, shift = affine[half]
+            scale, shift = scale_of[half], shift_of[half]
             planes = work.tile([P, PACK, ROWS], BF16, bufs=6)
             for u in range(PAIR):
                 pairs = norm_banks[group][:, u, :].bitcast(BF16).rearrange("p (n e) -> p n e", e=PAIR)
@@ -245,12 +249,13 @@ def tile_decoder_pb_e_kernel(tc, h7_pre, g7, be7, W8_words, W8_scales, b8, out):
                 stage(last_group // PASSES)
 
         for step in range(-LEAD, GROUPS + 7):
+            for_group(fill_norm_bank, step + 3)
             for_group(statistics, step + LEAD)
-            for_half(inverse_deviation, step + LEAD)
-            for_half(scale_and_shift, step + LEAD)
-            for_group(fill_norm_bank, step + 1)
+            for_half(scale_from_variance, step + LEAD)
+            for_half(scaled_mean, step + LEAD - 3)
             for_group(normalise, step)
             for_group(regroup, step - 1)
+            for_half(shift_from_mean, step + LEAD - 3)
             for_group(quantise, step - 3)
             for_block(multiply, step - 4)
             for_block(add_bias, step - 5)

@@ -37,8 +37,9 @@ def tile_decoder_pb_e_kernel(tc, h7_pre, g7, be7, W8_words, W8_scales, b8, out):
         small = ctx.enter_context(tc.tile_pool(name="small", bufs=8))
         work = ctx.enter_context(tc.tile_pool(name="work", bufs=3))
         psum_stats = ctx.enter_context(tc.psum_pool(name="psum_stats", bufs=2))
-        psum_norm = ctx.enter_context(tc.psum_pool(name="psum_norm", bufs=4))
-        psum_out = ctx.enter_context(tc.psum_pool(name="psum_out", bufs=2))
+        psum_scalar = ctx.enter_context(tc.psum_pool(name="psum_scalar", bufs=1))
+        psum_norm = ctx.enter_context(tc.psum_pool(name="psum_norm", bufs=3))
+        psum_out = ctx.enter_context(tc.psum_pool(name="psum_out", bufs=1))
         ctx.enter_context(tc.manual_schedule())
 
         w_planes = keep.tile([P, GROUPS, CHANNELS], U8, align_bytes=64)
@@ -47,6 +48,8 @@ def tile_decoder_pb_e_kernel(tc, h7_pre, g7, be7, W8_words, W8_scales, b8, out):
         nc.vector.memset(gain_rows[2 * GROUPS : P, :], 0.0)
         minus_half = keep.tile([P, HALF * PACK], F32)
         nc.vector.memset(minus_half[:], -0.5)
+        ones = keep.tile([P, 1], BF16)
+        nc.vector.memset(ones[:], 1.0)
         ident = keep.tile([P, P], F32)
         make_identity(nc, ident[:])
 
@@ -111,6 +114,8 @@ def tile_decoder_pb_e_kernel(tc, h7_pre, g7, be7, W8_words, W8_scales, b8, out):
         )
 
         moments = {}
+        scalar_banks = {}
+        sums_of = {}
         scale_of = {}
         mean_scaled_of = {}
         shift_of = {}
@@ -120,17 +125,67 @@ def tile_decoder_pb_e_kernel(tc, h7_pre, g7, be7, W8_words, W8_scales, b8, out):
         sums = {}
         logits_of = {}
 
+        def on_scalar(group):
+            return group % 3 == 2
+
         def statistics(group):
             b, g = divmod(group, PASSES)
             half, place = divmod(group, HALF)
             if place == 0:
                 moments_tile = small.tile([P, HALF * PAIR * 6], F32, name="moments")
                 moments[half] = moments_tile
+            if on_scalar(group):
+                bank = psum_scalar.tile([P, PAIR, ROWS], F32, name="scalar_bank")
+                transpose_group(bank, b, g)
+                scalar_banks[group] = bank
+                sums = psum_scalar.tile([P, PACK], F32, name="sums")
+                for t in range(PACK):
+                    for r in range(ROW_TILES):
+                        nc.tensor.matmul(
+                            out=sums[:, t : t + 1],
+                            lhsT=x_rows[(b, r)][:, K_PASS * g + t : K_PASS * (g + 1) : PACK],
+                            rhs=ones[:],
+                            start=(r == 0),
+                            stop=(r == ROW_TILES - 1),
+                        )
+                sums_of[group] = sums
+                return
             stat_bank = psum_stats.tile([P, PAIR, ROWS], F32, tag="stat_bank")
             transpose_group(stat_bank, b, g)
             for u in range(PAIR):
                 at = 6 * (PAIR * place + u)
                 nc.vector.bn_stats(out=moments[half][:, at : at + 6], in_=stat_bank[:, u, :].bitcast(BF16))
+
+        def means(group):
+            if not on_scalar(group):
+                return
+            half, place = divmod(group, HALF)
+            triples = moments[half][:].rearrange("p (f s) -> p f s", s=3)
+            nc.scalar.activation(
+                out=triples[:, PACK * place : PACK * (place + 1), 1],
+                in_=sums_of[group][:],
+                func=ACT.Copy,
+                scale=1.0 / ROWS,
+            )
+
+        def squared_deviations(group):
+            if not on_scalar(group):
+                return
+            half, place = divmod(group, HALF)
+            triples = moments[half][:].rearrange("p (f s) -> p f s", s=3)
+            for u in range(PAIR):
+                pairs = scalar_banks[group][:, u, :].bitcast(BF16).rearrange("p (n e) -> p n e", e=PAIR)
+                for e in range(PAIR):
+                    f = PACK * place + PAIR * u + e
+                    squares = work.tile([P, ROWS], BF16)
+                    nc.scalar.activation(
+                        out=squares[:],
+                        in_=pairs[:, :, e],
+                        func=ACT.Square,
+                        bias=triples[:, f : f + 1, 1],
+                        scale=-1.0,
+                        accum_out=triples[:, f : f + 1, 2],
+                    )
 
         def scale_from_variance(half):
             triples = moments[half][:].rearrange("p (f s) -> p f s", s=3)
@@ -190,10 +245,7 @@ def tile_decoder_pb_e_kernel(tc, h7_pre, g7, be7, W8_words, W8_scales, b8, out):
                 quantised[b] = (grouped, a_codes, a_planes)
             side_by_side = quantised[b][0][:, g].rearrange("p (c i) t -> p c t i", i=4)
             by_feature = planes_of[group][:].rearrange("p t (c i) -> p c t i", i=4)
-            if g == 0:
-                nc.scalar.copy(out=side_by_side, in_=by_feature)
-            else:
-                nc.vector.tensor_copy(out=side_by_side, in_=by_feature)
+            nc.vector.tensor_copy(out=side_by_side, in_=by_feature)
 
         def quantise(group):
             b, g = divmod(group, PASSES)
@@ -248,12 +300,14 @@ def tile_decoder_pb_e_kernel(tc, h7_pre, g7, be7, W8_words, W8_scales, b8, out):
             if 0 <= last_group < GROUPS and last_group % PASSES == PASSES - 1:
                 stage(last_group // PASSES)
 
-        for step in range(-LEAD, GROUPS + 7):
-            for_group(fill_norm_bank, step + 3)
-            for_group(statistics, step + LEAD)
+        for step in range(-LEAD - 2, GROUPS + 7):
+            for_group(statistics, step + LEAD + 2)
+            for_group(fill_norm_bank, step + 2)
             for_half(scale_from_variance, step + LEAD)
             for_half(scaled_mean, step + LEAD - 3)
+            for_group(means, step + LEAD + 1)
             for_group(normalise, step)
+            for_group(squared_deviations, step + LEAD + 1)
             for_group(regroup, step - 1)
             for_half(shift_from_mean, step + LEAD - 3)
             for_group(quantise, step - 3)

@@ -78,21 +78,23 @@ def tile_decoder_pb_e_kernel(tc, h7_pre, g7, be7, W8_words, W8_scales, b8, out):
         warm = keep.tile([P, 1], F32)
         nc.scalar.activation(out=warm[:], in_=minus_half[:, 0:1], func=ACT.Sigmoid)
 
-        load_x(0)
-        load_x(1)
+        for b in range(4):
+            load_x(b)
         load_w(0)
         scale_rows = W8_scales.rearrange("g (q r) c -> r q g c", r=4)
         for r in range(4):
             nc.sync.dma_start(out=w_planes[r:P:32, :, :].bitcast(I32), in_=scale_rows[r].bitcast(I32))
+        load_x(4)
         bias_all = keep.tile([P, BLOCKS, CHANNELS], BF16)
         nc.sync.dma_start(
             out=bias_all[:].rearrange("p b c -> p (b c)"),
             in_=b8.rearrange("b c -> (b c)").partition_broadcast(P),
         )
-        for b in range(2, BLOCKS):
+        for b in range(5, BLOCKS):
+            load_w(b - 4)
             load_x(b)
-            load_w(b - 1)
-        load_w(BLOCKS - 1)
+        for b in range(BLOCKS - 4, BLOCKS):
+            load_w(b)
 
         def transpose_group(bank, b, g):
             for r in range(ROW_TILES):

@@ -25,7 +25,7 @@ GROUPS = BLOCKS * PASSES
 PAIR = 2
 HALF = 2
 EPS = 1e-5
-LEAD = 8
+LEAD = 6
 
 FLOPS = 2 * BLOCKS * ROWS * FEATURES * CHANNELS
 
@@ -46,8 +46,8 @@ def tile_decoder_pb_e_kernel(tc, h7_pre, g7, be7, W8_words, W8_scales, b8, out):
         nc.vector.memset(w_planes[:].bitcast(I32), 0)
         gain_rows = keep.tile([P, K_PASS], BF16)
         nc.vector.memset(gain_rows[2 * GROUPS : P, :], 0.0)
-        minus_half = keep.tile([P, HALF * PACK], F32)
-        nc.vector.memset(minus_half[:], -0.5)
+        one = keep.tile([P, 1], F32)
+        nc.vector.memset(one[:], 1.0)
         ones = keep.tile([P, 1], BF16)
         nc.vector.memset(ones[:], 1.0)
         ident = keep.tile([P, P], F32)
@@ -76,7 +76,7 @@ def tile_decoder_pb_e_kernel(tc, h7_pre, g7, be7, W8_words, W8_scales, b8, out):
         nc.scalar.dma_start(out=gain_rows[0:GROUPS, :], in_=g7.rearrange("b (g k) -> (b g) k", g=PASSES))
         nc.scalar.dma_start(out=gain_rows[GROUPS : 2 * GROUPS, :], in_=be7.rearrange("b (g k) -> (b g) k", g=PASSES))
         warm = keep.tile([P, 1], F32)
-        nc.scalar.activation(out=warm[:], in_=minus_half[:, 0:1], func=ACT.Sigmoid)
+        nc.scalar.activation(out=warm[:], in_=one[:], func=ACT.Sqrt)
 
         for b in range(4):
             load_x(b)
@@ -119,7 +119,7 @@ def tile_decoder_pb_e_kernel(tc, h7_pre, g7, be7, W8_words, W8_scales, b8, out):
         scalar_banks = {}
         sums_of = {}
         scale_of = {}
-        mean_scaled_of = {}
+        std_of = {}
         shift_of = {}
         norm_banks = {}
         planes_of = {}
@@ -189,29 +189,25 @@ def tile_decoder_pb_e_kernel(tc, h7_pre, g7, be7, W8_words, W8_scales, b8, out):
                         accum_out=triples[:, f : f + 1, 2],
                     )
 
-        def scale_from_variance(half):
+        def deviation(half):
             triples = moments[half][:].rearrange("p (f s) -> p f s", s=3)
-            var_eps = small.tile([P, HALF * PACK], F32)
-            nc.gpsimd.tensor_scalar(
-                out=var_eps[:], in0=triples[:, :, 2], scalar1=1.0 / ROWS, scalar2=EPS, op0=ALU.mult, op1=ALU.add
-            )
+            std = small.tile([P, HALF * PACK], F32)
+            nc.scalar.activation(out=std[:], in_=triples[:, :, 2], func=ACT.Sqrt, bias=EPS, scale=1.0 / ROWS)
+            std_of[half] = std
+
+        def scale_and_shift(half):
+            triples = moments[half][:].rearrange("p (f s) -> p f s", s=3)
             rstd = small.tile([P, HALF * PACK], F32)
-            nc.gpsimd.tensor_tensor(out=rstd[:], in0=var_eps[:], in1=minus_half[:], op=ALU.pow)
+            nc.vector.reciprocal(out=rstd[:], in_=std_of[half][:])
             gain = gain_cols[:, HALF * half : HALF * (half + 1)].rearrange("p r u e -> p (r u e)")
             scale = small.tile([P, HALF * PACK], F32)
             nc.gpsimd.tensor_tensor(out=scale[:], in0=rstd[:], in1=gain, op=ALU.mult)
             scale_of[half] = scale
-
-        def scaled_mean(half):
-            triples = moments[half][:].rearrange("p (f s) -> p f s", s=3)
             mean_scaled = small.tile([P, HALF * PACK], F32)
-            nc.vector.tensor_tensor(out=mean_scaled[:], in0=triples[:, :, 1], in1=scale_of[half][:], op=ALU.mult)
-            mean_scaled_of[half] = mean_scaled
-
-        def shift_from_mean(half):
+            nc.gpsimd.tensor_tensor(out=mean_scaled[:], in0=triples[:, :, 1], in1=scale[:], op=ALU.mult)
             beta = gain_cols[:, GROUPS + HALF * half : GROUPS + HALF * (half + 1)].rearrange("p r u e -> p (r u e)")
             shift = small.tile([P, HALF * PACK], F32)
-            nc.vector.tensor_tensor(out=shift[:], in0=beta, in1=mean_scaled_of[half][:], op=ALU.subtract)
+            nc.gpsimd.tensor_tensor(out=shift[:], in0=beta, in1=mean_scaled[:], op=ALU.subtract)
             shift_of[half] = shift
 
         def fill_norm_bank(group):
@@ -276,7 +272,7 @@ def tile_decoder_pb_e_kernel(tc, h7_pre, g7, be7, W8_words, W8_scales, b8, out):
             sums[b] = acc
 
         def add_bias(b):
-            logits = work.tile([P, ROW_TILES, CHANNELS], F32)
+            logits = work.tile([P, ROW_TILES, CHANNELS], F32, bufs=BLOCKS)
             nc.vector.tensor_tensor(
                 out=logits[:],
                 in0=sums[b][:],
@@ -303,16 +299,17 @@ def tile_decoder_pb_e_kernel(tc, h7_pre, g7, be7, W8_words, W8_scales, b8, out):
                 stage(last_group // PASSES)
 
         for step in range(-LEAD - 2, GROUPS + 7):
+            for_half(scale_and_shift, step + LEAD - 1)
             for_group(statistics, step + LEAD + 2)
             for_group(fill_norm_bank, step + 2)
-            for_half(scale_from_variance, step + LEAD)
-            for_half(scaled_mean, step + LEAD - 3)
             for_group(means, step + LEAD + 1)
+            for_half(deviation, step + LEAD)
             for_group(normalise, step)
             for_group(squared_deviations, step + LEAD + 1)
             for_group(regroup, step - 1)
-            for_half(shift_from_mean, step + LEAD - 3)
             for_group(quantise, step - 3)
             for_block(multiply, step - 4)
             for_block(add_bias, step - 5)
-            for_block(squash_and_store, step - 6)
+            for b in range(BLOCKS):
+                if step == max(PASSES * b + PASSES - 1 + 6, GROUPS - LEAD + b):
+                    squash_and_store(b)

@@ -25,7 +25,7 @@ GROUPS = BLOCKS * PASSES
 PAIR = 2
 HALF = 2
 EPS = 1e-5
-LEAD = 6
+LEAD = 5
 
 FLOPS = 2 * BLOCKS * ROWS * FEATURES * CHANNELS
 
@@ -36,9 +36,8 @@ def tile_decoder_pb_e_kernel(tc, h7_pre, g7, be7, W8_words, W8_scales, b8, out):
         keep = ctx.enter_context(tc.tile_pool(name="keep", bufs=1))
         small = ctx.enter_context(tc.tile_pool(name="small", bufs=8))
         work = ctx.enter_context(tc.tile_pool(name="work", bufs=3))
-        psum_stats = ctx.enter_context(tc.psum_pool(name="psum_stats", bufs=2))
-        psum_scalar = ctx.enter_context(tc.psum_pool(name="psum_scalar", bufs=1))
-        psum_norm = ctx.enter_context(tc.psum_pool(name="psum_norm", bufs=3))
+        psum_x = ctx.enter_context(tc.psum_pool(name="psum_x", bufs=LEAD + 1))
+        psum_sums = ctx.enter_context(tc.psum_pool(name="psum_sums", bufs=1))
         psum_out = ctx.enter_context(tc.psum_pool(name="psum_out", bufs=1))
         ctx.enter_context(tc.manual_schedule())
 
@@ -106,7 +105,7 @@ def tile_decoder_pb_e_kernel(tc, h7_pre, g7, be7, W8_words, W8_scales, b8, out):
                         ident[:],
                     )
 
-        gain_bank = psum_stats.tile([P, PAIR, P], F32, tag="stat_bank")
+        gain_bank = psum_x.tile([P, PAIR, P], F32, tag="x_bank")
         for u in range(PAIR):
             nc.tensor.transpose(gain_bank[:, u, :], gain_rows[:].bitcast(F32)[:, u : K_PASS // PAIR : PAIR], ident[:])
         gain_cols = keep.tile([P, 2 * GROUPS, PAIR, PAIR], F32)
@@ -116,31 +115,30 @@ def tile_decoder_pb_e_kernel(tc, h7_pre, g7, be7, W8_words, W8_scales, b8, out):
         )
 
         moments = {}
-        scalar_banks = {}
+        x_banks = {}
         sums_of = {}
         scale_of = {}
         std_of = {}
         shift_of = {}
-        norm_banks = {}
         planes_of = {}
         quantised = {}
         sums = {}
         logits_of = {}
 
         def on_scalar(group):
-            return group % 3 == 2
+            return group % 6 in (0, 2)
 
-        def statistics(group):
+        def transpose(group):
             b, g = divmod(group, PASSES)
             half, place = divmod(group, HALF)
             if place == 0:
                 moments_tile = small.tile([P, HALF * PAIR * 6], F32, name="moments")
                 moments[half] = moments_tile
+            x_bank = psum_x.tile([P, PAIR, ROWS], F32, tag="x_bank")
+            transpose_group(x_bank, b, g)
+            x_banks[group] = x_bank
             if on_scalar(group):
-                bank = psum_scalar.tile([P, PAIR, ROWS], F32, name="scalar_bank")
-                transpose_group(bank, b, g)
-                scalar_banks[group] = bank
-                sums = psum_scalar.tile([P, PACK], F32, name="sums")
+                sums = psum_sums.tile([P, PACK], F32, name="sums")
                 for t in range(PACK):
                     for r in range(ROW_TILES):
                         nc.tensor.matmul(
@@ -151,12 +149,14 @@ def tile_decoder_pb_e_kernel(tc, h7_pre, g7, be7, W8_words, W8_scales, b8, out):
                             stop=(r == ROW_TILES - 1),
                         )
                 sums_of[group] = sums
+
+        def statistics(group):
+            if on_scalar(group):
                 return
-            stat_bank = psum_stats.tile([P, PAIR, ROWS], F32, tag="stat_bank")
-            transpose_group(stat_bank, b, g)
+            half, place = divmod(group, HALF)
             for u in range(PAIR):
                 at = 6 * (PAIR * place + u)
-                nc.vector.bn_stats(out=moments[half][:, at : at + 6], in_=stat_bank[:, u, :].bitcast(BF16))
+                nc.vector.bn_stats(out=moments[half][:, at : at + 6], in_=x_banks[group][:, u, :].bitcast(BF16))
 
         def means(group):
             if not on_scalar(group):
@@ -176,7 +176,7 @@ def tile_decoder_pb_e_kernel(tc, h7_pre, g7, be7, W8_words, W8_scales, b8, out):
             half, place = divmod(group, HALF)
             triples = moments[half][:].rearrange("p (f s) -> p f s", s=3)
             for u in range(PAIR):
-                pairs = scalar_banks[group][:, u, :].bitcast(BF16).rearrange("p (n e) -> p n e", e=PAIR)
+                pairs = x_banks[group][:, u, :].bitcast(BF16).rearrange("p (n e) -> p n e", e=PAIR)
                 for e in range(PAIR):
                     f = PACK * place + PAIR * u + e
                     squares = work.tile([P, ROWS], BF16)
@@ -210,18 +210,12 @@ def tile_decoder_pb_e_kernel(tc, h7_pre, g7, be7, W8_words, W8_scales, b8, out):
             nc.gpsimd.tensor_tensor(out=shift[:], in0=beta, in1=mean_scaled[:], op=ALU.subtract)
             shift_of[half] = shift
 
-        def fill_norm_bank(group):
-            b, g = divmod(group, PASSES)
-            norm_bank = psum_norm.tile([P, PAIR, ROWS], F32)
-            transpose_group(norm_bank, b, g)
-            norm_banks[group] = norm_bank
-
         def normalise(group):
             half, place = divmod(group, HALF)
             scale, shift = scale_of[half], shift_of[half]
             planes = work.tile([P, PACK, ROWS], BF16, bufs=6)
             for u in range(PAIR):
-                pairs = norm_banks[group][:, u, :].bitcast(BF16).rearrange("p (n e) -> p n e", e=PAIR)
+                pairs = x_banks[group][:, u, :].bitcast(BF16).rearrange("p (n e) -> p n e", e=PAIR)
                 for e in range(PAIR):
                     t = PAIR * u + e
                     f = PACK * place + t
@@ -298,18 +292,18 @@ def tile_decoder_pb_e_kernel(tc, h7_pre, g7, be7, W8_words, W8_scales, b8, out):
             if 0 <= last_group < GROUPS and last_group % PASSES == PASSES - 1:
                 stage(last_group // PASSES)
 
-        for step in range(-LEAD - 2, GROUPS + 7):
-            for_half(scale_and_shift, step + LEAD - 1)
-            for_group(statistics, step + LEAD + 2)
-            for_group(fill_norm_bank, step + 2)
-            for_group(means, step + LEAD + 1)
-            for_half(deviation, step + LEAD)
+        for step in range(-LEAD, GROUPS + 7):
+            for_half(scale_and_shift, step + LEAD - 2)
+            for_group(transpose, step + LEAD)
+            for_group(means, step + LEAD - 1)
             for_group(normalise, step)
-            for_group(squared_deviations, step + LEAD + 1)
+            for_group(squared_deviations, step + LEAD - 1)
+            for_half(deviation, step + LEAD - 1)
             for_group(regroup, step - 1)
             for_group(quantise, step - 3)
             for_block(multiply, step - 4)
             for_block(add_bias, step - 5)
+            for_group(statistics, step + LEAD)
             for b in range(BLOCKS):
-                if step == max(PASSES * b + PASSES - 1 + 6, GROUPS - LEAD + b):
+                if step == max(PASSES * b + PASSES - 1 + 6, GROUPS - LEAD + 2 + b):
                     squash_and_store(b)

@@ -27,6 +27,8 @@ HALF = 2
 EPS = 1e-5
 LEAD = 5
 
+LAST_BLOCK = GROUPS - PASSES
+
 FLOPS = 2 * BLOCKS * ROWS * FEATURES * CHANNELS
 
 
@@ -124,6 +126,7 @@ def tile_decoder_pb_e_kernel(tc, h7_pre, g7, be7, W8_words, W8_scales, b8, out):
         quantised = {}
         sums = {}
         logits_of = {}
+        last_sums = {}
 
         def on_scalar(group):
             return group % 6 in (0, 2)
@@ -134,9 +137,6 @@ def tile_decoder_pb_e_kernel(tc, h7_pre, g7, be7, W8_words, W8_scales, b8, out):
             if place == 0:
                 moments_tile = small.tile([P, HALF * PAIR * 6], F32, name="moments")
                 moments[half] = moments_tile
-            x_bank = psum_x.tile([P, PAIR, ROWS], F32, tag="x_bank")
-            transpose_group(x_bank, b, g)
-            x_banks[group] = x_bank
             if on_scalar(group):
                 sums = psum_sums.tile([P, PACK], F32, name="sums")
                 for t in range(PACK):
@@ -149,6 +149,9 @@ def tile_decoder_pb_e_kernel(tc, h7_pre, g7, be7, W8_words, W8_scales, b8, out):
                             stop=(r == ROW_TILES - 1),
                         )
                 sums_of[group] = sums
+            x_bank = psum_x.tile([P, PAIR, ROWS], F32, tag="x_bank")
+            transpose_group(x_bank, b, g)
+            x_banks[group] = x_bank
 
         def statistics(group):
             if on_scalar(group):
@@ -199,15 +202,16 @@ def tile_decoder_pb_e_kernel(tc, h7_pre, g7, be7, W8_words, W8_scales, b8, out):
             triples = moments[half][:].rearrange("p (f s) -> p f s", s=3)
             rstd = small.tile([P, HALF * PACK], F32)
             nc.vector.reciprocal(out=rstd[:], in_=std_of[half][:])
+            engine = nc.vector if half == 0 else nc.gpsimd
             gain = gain_cols[:, HALF * half : HALF * (half + 1)].rearrange("p r u e -> p (r u e)")
             scale = small.tile([P, HALF * PACK], F32)
-            nc.gpsimd.tensor_tensor(out=scale[:], in0=rstd[:], in1=gain, op=ALU.mult)
+            engine.tensor_tensor(out=scale[:], in0=rstd[:], in1=gain, op=ALU.mult)
             scale_of[half] = scale
             mean_scaled = small.tile([P, HALF * PACK], F32)
-            nc.gpsimd.tensor_tensor(out=mean_scaled[:], in0=triples[:, :, 1], in1=scale[:], op=ALU.mult)
+            engine.tensor_tensor(out=mean_scaled[:], in0=triples[:, :, 1], in1=scale[:], op=ALU.mult)
             beta = gain_cols[:, GROUPS + HALF * half : GROUPS + HALF * (half + 1)].rearrange("p r u e -> p (r u e)")
             shift = small.tile([P, HALF * PACK], F32)
-            nc.gpsimd.tensor_tensor(out=shift[:], in0=beta, in1=mean_scaled[:], op=ALU.subtract)
+            engine.tensor_tensor(out=shift[:], in0=beta, in1=mean_scaled[:], op=ALU.subtract)
             shift_of[half] = shift
 
         def normalise(group):
@@ -265,6 +269,34 @@ def tile_decoder_pb_e_kernel(tc, h7_pre, g7, be7, W8_words, W8_scales, b8, out):
                     )
             sums[b] = acc
 
+        def multiply_last(group):
+            b, g = divmod(group, PASSES)
+            grouped, a_codes, a_planes = quantised[b]
+            for r in range(ROW_TILES):
+                if g == 0:
+                    last_acc = psum_x.tile([P, CHANNELS], F32, tag="x_bank")
+                    last_sums[r] = last_acc
+                rows = slice(r * P, (r + 1) * P)
+                nc.tensor.matmul_mx(
+                    out=last_sums[r][:],
+                    lhsT=a_codes[:, g, rows].bitcast(FP8X4),
+                    lhsT_scale=a_planes[:, g, rows],
+                    rhs=w_words[b][:, g, :].bitcast(FP8X4),
+                    rhs_scale=w_planes[:, group, :],
+                    start=(g == 0),
+                    stop=(g == PASSES - 1),
+                )
+
+        def finish_last():
+            for r in range(ROW_TILES):
+                last_logits = work.tile([P, CHANNELS], F32, bufs=ROW_TILES)
+                nc.vector.tensor_tensor(
+                    out=last_logits[:], in0=last_sums[r][:], in1=bias_all[:, BLOCKS - 1, :], op=ALU.add
+                )
+                last_probs = work.tile([P, CHANNELS], F32, bufs=ROW_TILES)
+                nc.scalar.activation(out=last_probs[:], in_=last_logits[:], func=ACT.Sigmoid)
+                nc.sync.dma_start(out=out[r * P : (r + 1) * P, BLOCKS - 1, :], in_=last_probs[:])
+
         def add_bias(b):
             logits = work.tile([P, ROW_TILES, CHANNELS], F32, bufs=BLOCKS)
             nc.vector.tensor_tensor(
@@ -300,10 +332,17 @@ def tile_decoder_pb_e_kernel(tc, h7_pre, g7, be7, W8_words, W8_scales, b8, out):
             for_group(squared_deviations, step + LEAD - 1)
             for_half(deviation, step + LEAD - 1)
             for_group(regroup, step - 1)
-            for_group(quantise, step - 3)
-            for_block(multiply, step - 4)
-            for_block(add_bias, step - 5)
+            if step - 3 < LAST_BLOCK:
+                for_group(quantise, step - 3)
+            if step - 4 < LAST_BLOCK:
+                for_block(multiply, step - 4)
+            if step - 5 < LAST_BLOCK:
+                for_block(add_bias, step - 5)
+            if step - 1 >= LAST_BLOCK:
+                for_group(quantise, step - 1)
+                for_group(multiply_last, step - 1)
             for_group(statistics, step + LEAD)
-            for b in range(BLOCKS):
+            for b in range(BLOCKS - 1):
                 if step == max(PASSES * b + PASSES - 1 + 6, GROUPS - LEAD + 2 + b):
                     squash_and_store(b)
+        finish_last()

@@ -77,7 +77,7 @@ def tile_decoder_pb_e_kernel(tc, h7_pre, g7, be7, W8_words, W8_scales, b8, out):
         nc.scalar.dma_start(out=gain_rows[0:GROUPS, :], in_=g7.rearrange("b (g k) -> (b g) k", g=PASSES))
         nc.scalar.dma_start(out=gain_rows[GROUPS : 2 * GROUPS, :], in_=be7.rearrange("b (g k) -> (b g) k", g=PASSES))
         warm = keep.tile([P, 1], F32)
-        nc.scalar.activation(out=warm[:], in_=one[:], func=ACT.Sqrt)
+        nc.scalar.activation(out=warm[:], in_=one[:], func=ACT.Abs_reciprocal_sqrt)
 
         for b in range(4):
             load_x(b)
@@ -120,7 +120,7 @@ def tile_decoder_pb_e_kernel(tc, h7_pre, g7, be7, W8_words, W8_scales, b8, out):
         x_banks = {}
         sums_of = {}
         scale_of = {}
-        std_of = {}
+        rstd_of = {}
         shift_of = {}
         planes_of = {}
         quantised = {}
@@ -194,14 +194,15 @@ def tile_decoder_pb_e_kernel(tc, h7_pre, g7, be7, W8_words, W8_scales, b8, out):
 
         def deviation(half):
             triples = moments[half][:].rearrange("p (f s) -> p f s", s=3)
-            std = small.tile([P, HALF * PACK], F32)
-            nc.scalar.activation(out=std[:], in_=triples[:, :, 2], func=ACT.Sqrt, bias=EPS, scale=1.0 / ROWS)
-            std_of[half] = std
+            rstd = small.tile([P, HALF * PACK], F32)
+            nc.scalar.activation(
+                out=rstd[:], in_=triples[:, :, 2], func=ACT.Abs_reciprocal_sqrt, bias=EPS, scale=1.0 / ROWS
+            )
+            rstd_of[half] = rstd
 
         def scale_and_shift(half):
             triples = moments[half][:].rearrange("p (f s) -> p f s", s=3)
-            rstd = small.tile([P, HALF * PACK], F32)
-            nc.vector.reciprocal(out=rstd[:], in_=std_of[half][:])
+            rstd = rstd_of[half]
             engine = nc.vector if half == 0 else nc.gpsimd
             gain = gain_cols[:, HALF * half : HALF * (half + 1)].rearrange("p r u e -> p (r u e)")
             scale = small.tile([P, HALF * PACK], F32)

@@ -43,15 +43,17 @@ def tile_decoder_pb_e_kernel(tc, h7_pre, g7, be7, W8_words, W8_scales, b8, out):
         psum_out = ctx.enter_context(tc.psum_pool(name="psum_out", bufs=1))
         ctx.enter_context(tc.manual_schedule())
 
-        w_planes = keep.tile([P, GROUPS, CHANNELS], U8, align_bytes=64)
-        nc.vector.memset(w_planes[:].bitcast(I32), 0)
         gain_rows = keep.tile([P, K_PASS], BF16)
         nc.vector.memset(gain_rows[2 * GROUPS : P, :], 0.0)
         one = keep.tile([P, 1], F32)
         nc.vector.memset(one[:], 1.0)
         ones = keep.tile([P, 1], BF16)
         nc.vector.memset(ones[:], 1.0)
-        ident = keep.tile([P, P], F32)
+        w_planes = keep.tile([P, GROUPS, CHANNELS], U8, align_bytes=64)
+        nc.vector.memset(w_planes[:].bitcast(I32), 0)
+        ident_f32 = keep.tile([P, P], F32)
+        make_identity(nc, ident_f32[:])
+        ident = keep.tile([P, P], BF16)
         make_identity(nc, ident[:])
 
         x_rows = {}
@@ -97,19 +99,9 @@ def tile_decoder_pb_e_kernel(tc, h7_pre, g7, be7, W8_words, W8_scales, b8, out):
         for b in range(BLOCKS - 4, BLOCKS):
             load_w(b)
 
-        def transpose_group(bank, b, g):
-            for r in range(ROW_TILES):
-                words = x_rows[(b, r)][:].bitcast(F32)
-                for u in range(PAIR):
-                    nc.tensor.transpose(
-                        bank[:, u, r * P : (r + 1) * P],
-                        words[:, (K_PASS // PAIR) * g + u : (K_PASS // PAIR) * (g + 1) : PAIR],
-                        ident[:],
-                    )
-
         gain_bank = psum_x.tile([P, PAIR, P], F32, tag="x_bank")
         for u in range(PAIR):
-            nc.tensor.transpose(gain_bank[:, u, :], gain_rows[:].bitcast(F32)[:, u : K_PASS // PAIR : PAIR], ident[:])
+            nc.tensor.transpose(gain_bank[:, u, :], gain_rows[:].bitcast(F32)[:, u : K_PASS // PAIR : PAIR], ident_f32[:])
         gain_cols = keep.tile([P, 2 * GROUPS, PAIR, PAIR], F32)
         nc.vector.tensor_copy(
             out=gain_cols[:],
@@ -118,7 +110,6 @@ def tile_decoder_pb_e_kernel(tc, h7_pre, g7, be7, W8_words, W8_scales, b8, out):
 
         moments = {}
         x_banks = {}
-        sums_of = {}
         scale_of = {}
         rstd_of = {}
         shift_of = {}
@@ -129,7 +120,39 @@ def tile_decoder_pb_e_kernel(tc, h7_pre, g7, be7, W8_words, W8_scales, b8, out):
         last_sums = {}
 
         def on_scalar(group):
-            return group % 6 in (0, 2)
+            return group not in (1, 3)
+
+        def norm_on_scalar(group):
+            return group in (GROUPS - 4, GROUPS - 2)
+
+        def sums_work(half):
+            sums = sums_bank[:, half % 2]
+
+            def one(place, t, r):
+                b, g = divmod(HALF * half + place, PASSES)
+                f = PACK * place + t
+                nc.tensor.matmul(
+                    out=sums[:, f : f + 1],
+                    lhsT=x_rows[(b, r)][:, K_PASS * g + t : K_PASS * (g + 1) : PACK],
+                    rhs=ones[:],
+                    start=(r == 0),
+                    stop=(r == ROW_TILES - 1),
+                )
+
+            return [
+                (one, place, t, r)
+                for place in range(HALF)
+                if on_scalar(HALF * half + place)
+                for t in range(PACK)
+                for r in range(ROW_TILES)
+            ]
+
+        def run(calls):
+            for call in calls:
+                call[0](call[1], call[2], call[3])
+
+        sums_bank = psum_sums.tile([P, 2, HALF * PACK], F32, name="sums")
+        pending = []
 
         def transpose(group):
             b, g = divmod(group, PASSES)
@@ -137,20 +160,20 @@ def tile_decoder_pb_e_kernel(tc, h7_pre, g7, be7, W8_words, W8_scales, b8, out):
             if place == 0:
                 moments_tile = small.tile([P, HALF * PAIR * 6], F32, name="moments")
                 moments[half] = moments_tile
-            if on_scalar(group):
-                sums = psum_sums.tile([P, PACK], F32, name="sums")
-                for t in range(PACK):
-                    for r in range(ROW_TILES):
-                        nc.tensor.matmul(
-                            out=sums[:, t : t + 1],
-                            lhsT=x_rows[(b, r)][:, K_PASS * g + t : K_PASS * (g + 1) : PACK],
-                            rhs=ones[:],
-                            start=(r == 0),
-                            stop=(r == ROW_TILES - 1),
-                        )
-                sums_of[group] = sums
-            x_bank = psum_x.tile([P, PAIR, ROWS], F32, tag="x_bank")
-            transpose_group(x_bank, b, g)
+                if half < 2:
+                    run(sums_work(half))
+                if 1 <= half < GROUPS // HALF - 1:
+                    pending.extend(sums_work(half + 1))
+            x_bank = psum_x.tile([P, PACK, ROWS], BF16, tag="x_bank")
+            for t in range(PACK):
+                for r in range(ROW_TILES):
+                    nc.tensor.transpose(
+                        x_bank[:, t, r * P : (r + 1) * P],
+                        x_rows[(b, r)][:, K_PASS * g + t : K_PASS * (g + 1) : PACK],
+                        ident[:],
+                    )
+                    run(pending[:2])
+                    pending[:2] = []
             x_banks[group] = x_bank
 
         def statistics(group):
@@ -159,16 +182,19 @@ def tile_decoder_pb_e_kernel(tc, h7_pre, g7, be7, W8_words, W8_scales, b8, out):
             half, place = divmod(group, HALF)
             for u in range(PAIR):
                 at = 6 * (PAIR * place + u)
-                nc.vector.bn_stats(out=moments[half][:, at : at + 6], in_=x_banks[group][:, u, :].bitcast(BF16))
+                nc.vector.bn_stats(out=moments[half][:, at : at + 6], in_=x_banks[group][:, PAIR * u : PAIR * (u + 1), :].rearrange("p e n -> p n e"))
 
         def means(group):
-            if not on_scalar(group):
-                return
             half, place = divmod(group, HALF)
+            first = 0 if on_scalar(HALF * half) else 1
+            last = HALF if on_scalar(HALF * half + 1) else 1
+            if place != 0 or first >= last:
+                return
+            columns = slice(PACK * first, PACK * last)
             triples = moments[half][:].rearrange("p (f s) -> p f s", s=3)
             nc.scalar.activation(
-                out=triples[:, PACK * place : PACK * (place + 1), 1],
-                in_=sums_of[group][:],
+                out=triples[:, columns, 1],
+                in_=sums_bank[:, half % 2, columns],
                 func=ACT.Copy,
                 scale=1.0 / ROWS,
             )
@@ -178,19 +204,17 @@ def tile_decoder_pb_e_kernel(tc, h7_pre, g7, be7, W8_words, W8_scales, b8, out):
                 return
             half, place = divmod(group, HALF)
             triples = moments[half][:].rearrange("p (f s) -> p f s", s=3)
-            for u in range(PAIR):
-                pairs = x_banks[group][:, u, :].bitcast(BF16).rearrange("p (n e) -> p n e", e=PAIR)
-                for e in range(PAIR):
-                    f = PACK * place + PAIR * u + e
-                    squares = work.tile([P, ROWS], BF16)
-                    nc.scalar.activation(
-                        out=squares[:],
-                        in_=pairs[:, :, e],
-                        func=ACT.Square,
-                        bias=triples[:, f : f + 1, 1],
-                        scale=-1.0,
-                        accum_out=triples[:, f : f + 1, 2],
-                    )
+            for t in range(PACK):
+                f = PACK * place + t
+                squares = work.tile([P, ROWS], BF16)
+                nc.scalar.activation(
+                    out=squares[:],
+                    in_=x_banks[group][:, t, :],
+                    func=ACT.Square,
+                    bias=triples[:, f : f + 1, 1],
+                    scale=-1.0,
+                    accum_out=triples[:, f : f + 1, 2],
+                )
 
         def deviation(half):
             triples = moments[half][:].rearrange("p (f s) -> p f s", s=3)
@@ -219,17 +243,24 @@ def tile_decoder_pb_e_kernel(tc, h7_pre, g7, be7, W8_words, W8_scales, b8, out):
             half, place = divmod(group, HALF)
             scale, shift = scale_of[half], shift_of[half]
             planes = work.tile([P, PACK, ROWS], BF16, bufs=6)
-            for u in range(PAIR):
-                pairs = x_banks[group][:, u, :].bitcast(BF16).rearrange("p (n e) -> p n e", e=PAIR)
-                for e in range(PAIR):
-                    t = PAIR * u + e
-                    f = PACK * place + t
+            for t in range(PACK):
+                f = PACK * place + t
+                if norm_on_scalar(group):
                     nc.scalar.activation(
                         out=planes[:, t, :],
-                        in_=pairs[:, :, e],
-                        func=ACT.Relu,
+                        in_=x_banks[group][:, t, :],
+                        func=ACT.Identity,
                         bias=shift[:, f : f + 1],
                         scale=scale[:, f : f + 1],
+                    )
+                else:
+                    nc.vector.tensor_scalar(
+                        out=planes[:, t, :],
+                        in0=x_banks[group][:, t, :],
+                        scalar1=scale[:, f : f + 1],
+                        scalar2=shift[:, f : f + 1],
+                        op0=ALU.mult,
+                        op1=ALU.add,
                     )
             planes_of[group] = planes
 
@@ -242,7 +273,7 @@ def tile_decoder_pb_e_kernel(tc, h7_pre, g7, be7, W8_words, W8_scales, b8, out):
                 quantised[b] = (grouped, a_codes, a_planes)
             side_by_side = quantised[b][0][:, g].rearrange("p (c i) t -> p c t i", i=4)
             by_feature = planes_of[group][:].rearrange("p t (c i) -> p c t i", i=4)
-            nc.vector.tensor_copy(out=side_by_side, in_=by_feature)
+            nc.vector.tensor_scalar_max(side_by_side, by_feature, 0.0)
 
         def quantise(group):
             b, g = divmod(group, PASSES)

@@ -25,6 +25,7 @@ GROUPS = BLOCKS * PASSES
 PAIR = 2
 HALF = 2
 EPS = 1e-5
+WARM = 4
 LEAD = 5
 
 LAST_BLOCK = GROUPS - PASSES
@@ -43,6 +44,8 @@ def tile_decoder_pb_e_kernel(tc, h7_pre, g7, be7, W8_words, W8_scales, b8, out):
         psum_out = ctx.enter_context(tc.psum_pool(name="psum_out", bufs=1))
         ctx.enter_context(tc.manual_schedule())
 
+        wide = keep.tile([P, K_PASS], BF16)
+        nc.vector.memset(wide[:], 0.0)
         gain_rows = keep.tile([P, K_PASS], BF16)
         nc.vector.memset(gain_rows[2 * GROUPS : P, :], 0.0)
         one = keep.tile([P, 1], F32)
@@ -63,8 +66,9 @@ def tile_decoder_pb_e_kernel(tc, h7_pre, g7, be7, W8_words, W8_scales, b8, out):
             for r in range(ROW_TILES):
                 x_tile = keep.tile([P, FEATURES], BF16, name="x_%d_%d" % (b, r))
                 x_rows[(b, r)] = x_tile
-            for first in range(0, FEATURES, HALF * K_PASS):
-                cols = slice(first, first + HALF * K_PASS)
+            width = K_PASS if b == 0 else HALF * K_PASS
+            for first in range(0, FEATURES, width):
+                cols = slice(first, first + width)
                 for r in range(ROW_TILES):
                     nc.sync.dma_start(out=x_rows[(b, r)][:, cols], in_=h7_pre[b, r * P : (r + 1) * P, cols])
 
@@ -99,14 +103,22 @@ def tile_decoder_pb_e_kernel(tc, h7_pre, g7, be7, W8_words, W8_scales, b8, out):
         for b in range(BLOCKS - 4, BLOCKS):
             load_w(b)
 
-        gain_bank = psum_x.tile([P, PAIR, P], F32, tag="x_bank")
-        for u in range(PAIR):
-            nc.tensor.transpose(gain_bank[:, u, :], gain_rows[:].bitcast(F32)[:, u : K_PASS // PAIR : PAIR], ident_f32[:])
         gain_cols = keep.tile([P, 2 * GROUPS, PAIR, PAIR], F32)
-        nc.vector.tensor_copy(
-            out=gain_cols[:],
-            in_=gain_bank[:].bitcast(BF16).rearrange("p u (r e) -> p r u e", e=PAIR)[:, 0 : 2 * GROUPS],
-        )
+
+        def transpose_gains():
+            gain_bank = psum_out.tile([P, PAIR, ROWS], F32, tag="product")
+            for u in range(PAIR):
+                nc.tensor.transpose(
+                    gain_bank[:, u, 0:P], gain_rows[:].bitcast(F32)[:, u : K_PASS // PAIR : PAIR], ident_f32[:]
+                )
+            nc.vector.tensor_copy(
+                out=gain_cols[:],
+                in_=gain_bank[:, :, 0:P].bitcast(BF16).rearrange("p u (r e) -> p r u e", e=PAIR)[:, 0 : 2 * GROUPS],
+            )
+
+        warm_bank = psum_out.tile([P, K_PASS], F32, tag="product")
+        for i in range(WARM):
+            nc.tensor.matmul(out=warm_bank[:], lhsT=wide[:, 0:P], rhs=wide[:], start=True, stop=True)
 
         moments = {}
         x_banks = {}
@@ -120,12 +132,12 @@ def tile_decoder_pb_e_kernel(tc, h7_pre, g7, be7, W8_words, W8_scales, b8, out):
         last_sums = {}
 
         def on_scalar(group):
-            return group not in (1, 3)
+            return group not in (0, HALF)
 
         def norm_on_scalar(group):
             return group in (GROUPS - 4, GROUPS - 2)
 
-        def sums_work(half):
+        def sums_work(half, places):
             sums = sums_bank[:, half % 2]
 
             def one(place, t, r):
@@ -141,7 +153,7 @@ def tile_decoder_pb_e_kernel(tc, h7_pre, g7, be7, W8_words, W8_scales, b8, out):
 
             return [
                 (one, place, t, r)
-                for place in range(HALF)
+                for place in places
                 if on_scalar(HALF * half + place)
                 for t in range(PACK)
                 for r in range(ROW_TILES)
@@ -160,10 +172,10 @@ def tile_decoder_pb_e_kernel(tc, h7_pre, g7, be7, W8_words, W8_scales, b8, out):
             if place == 0:
                 moments_tile = small.tile([P, HALF * PAIR * 6], F32, name="moments")
                 moments[half] = moments_tile
-                if half < 2:
-                    run(sums_work(half))
-                if 1 <= half < GROUPS // HALF - 1:
-                    pending.extend(sums_work(half + 1))
+            if half < 2:
+                run(sums_work(half, [place]))
+            if 1 <= half < GROUPS // HALF - 1 and place == (1 if half == 1 else 0):
+                pending.extend(sums_work(half + 1, range(HALF)))
             x_bank = psum_x.tile([P, PACK, ROWS], BF16, tag="x_bank")
             for t in range(PACK):
                 for r in range(ROW_TILES):
@@ -186,10 +198,10 @@ def tile_decoder_pb_e_kernel(tc, h7_pre, g7, be7, W8_words, W8_scales, b8, out):
 
         def means(group):
             half, place = divmod(group, HALF)
-            first = 0 if on_scalar(HALF * half) else 1
-            last = HALF if on_scalar(HALF * half + 1) else 1
-            if place != 0 or first >= last:
+            if not on_scalar(group) or (place == 1 and on_scalar(group - 1)):
                 return
+            first = place
+            last = HALF if on_scalar(HALF * half + 1) else 1
             columns = slice(PACK * first, PACK * last)
             triples = moments[half][:].rearrange("p (f s) -> p f s", s=3)
             nc.scalar.activation(
@@ -286,7 +298,7 @@ def tile_decoder_pb_e_kernel(tc, h7_pre, g7, be7, W8_words, W8_scales, b8, out):
 
         def multiply(b):
             grouped, a_codes, a_planes = quantised[b]
-            acc = psum_out.tile([P, ROW_TILES, CHANNELS], F32)
+            acc = psum_out.tile([P, ROW_TILES, CHANNELS], F32, tag="product")
             for r in range(ROW_TILES):
                 rows = slice(r * P, (r + 1) * P)
                 for g in range(PASSES):
@@ -358,8 +370,8 @@ def tile_decoder_pb_e_kernel(tc, h7_pre, g7, be7, W8_words, W8_scales, b8, out):
 
         for step in range(-LEAD, GROUPS + 7):
             for_half(scale_and_shift, step + LEAD - 2)
-            for_group(transpose, step + LEAD)
             for_group(means, step + LEAD - 1)
+            for_group(transpose, step + LEAD)
             for_group(normalise, step)
             for_group(squared_deviations, step + LEAD - 1)
             for_half(deviation, step + LEAD - 1)
@@ -374,6 +386,8 @@ def tile_decoder_pb_e_kernel(tc, h7_pre, g7, be7, W8_words, W8_scales, b8, out):
                 for_group(quantise, step - 1)
                 for_group(multiply_last, step - 1)
             for_group(statistics, step + LEAD)
+            if step + LEAD == HALF - 1:
+                transpose_gains()
             for b in range(BLOCKS - 1):
                 if step == max(PASSES * b + PASSES - 1 + 6, GROUPS - LEAD + 2 + b):
                     squash_and_store(b)

@@ -135,7 +135,7 @@ def tile_decoder_pb_e_kernel(tc, h7_pre, g7, be7, W8_words, W8_scales, b8, out):
             return group not in (0, HALF)
 
         def norm_on_scalar(group):
-            return group in (GROUPS - 4, GROUPS - 2)
+            return group == GROUPS - 3
 
         def sums_work(half, places):
             sums = sums_bank[:, half % 2]
@@ -164,7 +164,6 @@ def tile_decoder_pb_e_kernel(tc, h7_pre, g7, be7, W8_words, W8_scales, b8, out):
                 call[0](call[1], call[2], call[3])
 
         sums_bank = psum_sums.tile([P, 2, HALF * PACK], F32, name="sums")
-        pending = []
 
         def transpose(group):
             b, g = divmod(group, PASSES)
@@ -175,7 +174,7 @@ def tile_decoder_pb_e_kernel(tc, h7_pre, g7, be7, W8_words, W8_scales, b8, out):
             if half < 2:
                 run(sums_work(half, [place]))
             if 1 <= half < GROUPS // HALF - 1 and place == (1 if half == 1 else 0):
-                pending.extend(sums_work(half + 1, range(HALF)))
+                run(sums_work(half + 1, range(HALF)))
             x_bank = psum_x.tile([P, PACK, ROWS], BF16, tag="x_bank")
             for t in range(PACK):
                 for r in range(ROW_TILES):
@@ -184,8 +183,6 @@ def tile_decoder_pb_e_kernel(tc, h7_pre, g7, be7, W8_words, W8_scales, b8, out):
                         x_rows[(b, r)][:, K_PASS * g + t : K_PASS * (g + 1) : PACK],
                         ident[:],
                     )
-                    run(pending[:2])
-                    pending[:2] = []
             x_banks[group] = x_bank
 
         def statistics(group):
@@ -371,17 +368,17 @@ def tile_decoder_pb_e_kernel(tc, h7_pre, g7, be7, W8_words, W8_scales, b8, out):
         for step in range(-LEAD, GROUPS + 7):
             for_half(scale_and_shift, step + LEAD - 2)
             for_group(means, step + LEAD - 1)
+            if step - 2 < LAST_BLOCK:
+                for_group(quantise, step - 2)
+            for_group(regroup, step - 1)
             for_group(transpose, step + LEAD)
             for_group(normalise, step)
             for_group(squared_deviations, step + LEAD - 1)
             for_half(deviation, step + LEAD - 1)
-            for_group(regroup, step - 1)
             if step - 3 < LAST_BLOCK:
-                for_group(quantise, step - 3)
-            if step - 4 < LAST_BLOCK:
-                for_block(multiply, step - 4)
-            if step - 5 < LAST_BLOCK:
-                for_block(add_bias, step - 5)
+                for_block(multiply, step - 3)
+            if step - 6 < LAST_BLOCK:
+                for_block(add_bias, step - 6)
             if step - 1 >= LAST_BLOCK:
                 for_group(quantise, step - 1)
                 for_group(multiply_last, step - 1)
@@ -389,6 +386,6 @@ def tile_decoder_pb_e_kernel(tc, h7_pre, g7, be7, W8_words, W8_scales, b8, out):
             if step + LEAD == HALF - 1:
                 transpose_gains()
             for b in range(BLOCKS - 1):
-                if step == max(PASSES * b + PASSES - 1 + 6, GROUPS - LEAD + 2 + b):
+                if step == max(PASSES * b + PASSES - 1 + 7, GROUPS - LEAD + 2 + b):
                     squash_and_store(b)
         finish_last()

@@ -164,6 +164,7 @@ def tile_decoder_pb_e_kernel(tc, h7_pre, g7, be7, W8_words, W8_scales, b8, out):
                 call[0](call[1], call[2], call[3])
 
         sums_bank = psum_sums.tile([P, 2, HALF * PACK], F32, name="sums")
+        pending = []
 
         def transpose(group):
             b, g = divmod(group, PASSES)
@@ -174,7 +175,7 @@ def tile_decoder_pb_e_kernel(tc, h7_pre, g7, be7, W8_words, W8_scales, b8, out):
             if half < 2:
                 run(sums_work(half, [place]))
             if 1 <= half < GROUPS // HALF - 1 and place == (1 if half == 1 else 0):
-                run(sums_work(half + 1, range(HALF)))
+                pending.extend(sums_work(half + 1, range(HALF)))
             x_bank = psum_x.tile([P, PACK, ROWS], BF16, tag="x_bank")
             for t in range(PACK):
                 for r in range(ROW_TILES):
@@ -183,6 +184,8 @@ def tile_decoder_pb_e_kernel(tc, h7_pre, g7, be7, W8_words, W8_scales, b8, out):
                         x_rows[(b, r)][:, K_PASS * g + t : K_PASS * (g + 1) : PACK],
                         ident[:],
                     )
+                    run(pending[:2])
+                    pending[:2] = []
             x_banks[group] = x_bank
 
         def statistics(group):

@@ -127,7 +127,7 @@ def tile_decoder_pb_e_kernel(tc, h7_pre, g7, be7, W8_words, W8_scales, b8, out):
         shift_of = {}
         planes_of = {}
         quantised = {}
-        sums = {}
+        products = {}
         logits_of = {}
         last_sums = {}
 
@@ -184,8 +184,8 @@ def tile_decoder_pb_e_kernel(tc, h7_pre, g7, be7, W8_words, W8_scales, b8, out):
                         x_rows[(b, r)][:, K_PASS * g + t : K_PASS * (g + 1) : PACK],
                         ident[:],
                     )
-                    run(pending[:2])
-                    pending[:2] = []
+                    run(pending[:3])
+                    pending[:3] = []
             x_banks[group] = x_bank
 
         def statistics(group):
@@ -251,20 +251,38 @@ def tile_decoder_pb_e_kernel(tc, h7_pre, g7, be7, W8_words, W8_scales, b8, out):
             engine.tensor_tensor(out=shift[:], in0=beta, in1=mean_scaled[:], op=ALU.subtract)
             shift_of[half] = shift
 
+        def scalar_planes(group):
+            return 1 if group % PASSES == PASSES - 1 and PASSES <= group < LAST_BLOCK else 0
+
+        def planes_tile(group):
+            if group not in planes_of:
+                planes = work.tile([P, PACK, ROWS], BF16, bufs=7)
+                planes_of[group] = planes
+            return planes_of[group]
+
+        def normalise_on_scalar(group, t):
+            half, place = divmod(group, HALF)
+            f = PACK * place + t
+            nc.scalar.activation(
+                out=planes_tile(group)[:, t, :],
+                in_=x_banks[group][:, t, :],
+                func=ACT.Identity,
+                bias=shift_of[half][:, f : f + 1],
+                scale=scale_of[half][:, f : f + 1],
+            )
+
+        def help_normalise(group):
+            for t in range(scalar_planes(group)):
+                normalise_on_scalar(group, t)
+
         def normalise(group):
             half, place = divmod(group, HALF)
             scale, shift = scale_of[half], shift_of[half]
-            planes = work.tile([P, PACK, ROWS], BF16, bufs=6)
-            for t in range(PACK):
+            planes = planes_tile(group)
+            for t in range(scalar_planes(group), PACK):
                 f = PACK * place + t
                 if norm_on_scalar(group):
-                    nc.scalar.activation(
-                        out=planes[:, t, :],
-                        in_=x_banks[group][:, t, :],
-                        func=ACT.Identity,
-                        bias=shift[:, f : f + 1],
-                        scale=scale[:, f : f + 1],
-                    )
+                    normalise_on_scalar(group, t)
                 else:
                     nc.vector.tensor_scalar(
                         out=planes[:, t, :],
@@ -274,7 +292,6 @@ def tile_decoder_pb_e_kernel(tc, h7_pre, g7, be7, W8_words, W8_scales, b8, out):
                         op0=ALU.mult,
                         op1=ALU.add,
                     )
-            planes_of[group] = planes
 
         def regroup(group):
             b, g = divmod(group, PASSES)
@@ -296,22 +313,22 @@ def tile_decoder_pb_e_kernel(tc, h7_pre, g7, be7, W8_words, W8_scales, b8, out):
                 in_=grouped[:, g].rearrange("p n t -> p (n t)"),
             )
 
-        def multiply(b):
+        def multiply(b, r):
             grouped, a_codes, a_planes = quantised[b]
-            acc = psum_out.tile([P, ROW_TILES, CHANNELS], F32, tag="product")
-            for r in range(ROW_TILES):
-                rows = slice(r * P, (r + 1) * P)
-                for g in range(PASSES):
-                    nc.tensor.matmul_mx(
-                        out=acc[:, r, :],
-                        lhsT=a_codes[:, g, rows].bitcast(FP8X4),
-                        lhsT_scale=a_planes[:, g, rows],
-                        rhs=w_words[b][:, g, :].bitcast(FP8X4),
-                        rhs_scale=w_planes[:, PASSES * b + g, :],
-                        start=(g == 0),
-                        stop=(g == PASSES - 1),
-                    )
-            sums[b] = acc
+            if r == 0:
+                product = psum_out.tile([P, ROW_TILES, CHANNELS], F32, tag="product")
+                products[b] = product
+            rows = slice(r * P, (r + 1) * P)
+            for g in range(PASSES):
+                nc.tensor.matmul_mx(
+                    out=products[b][:, r, :],
+                    lhsT=a_codes[:, g, rows].bitcast(FP8X4),
+                    lhsT_scale=a_planes[:, g, rows],
+                    rhs=w_words[b][:, g, :].bitcast(FP8X4),
+                    rhs_scale=w_planes[:, PASSES * b + g, :],
+                    start=(g == 0),
+                    stop=(g == PASSES - 1),
+                )
 
         def multiply_last(group):
             b, g = divmod(group, PASSES)
@@ -345,7 +362,7 @@ def tile_decoder_pb_e_kernel(tc, h7_pre, g7, be7, W8_words, W8_scales, b8, out):
             logits = work.tile([P, ROW_TILES, CHANNELS], F32, bufs=BLOCKS)
             nc.vector.tensor_tensor(
                 out=logits[:],
-                in0=sums[b][:],
+                in0=products[b][:],
                 in1=bias_all[:, b, :].unsqueeze(1).to_broadcast([P, ROW_TILES, CHANNELS]),
                 op=ALU.add,
             )
@@ -369,17 +386,23 @@ def tile_decoder_pb_e_kernel(tc, h7_pre, g7, be7, W8_words, W8_scales, b8, out):
                 stage(last_group // PASSES)
 
         for step in range(-LEAD, GROUPS + 7):
-            for_half(scale_and_shift, step + LEAD - 2)
             for_group(means, step + LEAD - 1)
+            if step + LEAD - 2 >= PASSES:
+                for_half(deviation, step + LEAD - 2)
+            for_half(scale_and_shift, step + LEAD - 2)
             if step - 2 < LAST_BLOCK:
                 for_group(quantise, step - 2)
             for_group(regroup, step - 1)
             for_group(transpose, step + LEAD)
             for_group(normalise, step)
+            for_group(help_normalise, step + 1)
             for_group(squared_deviations, step + LEAD - 1)
-            for_half(deviation, step + LEAD - 1)
-            if step - 3 < LAST_BLOCK:
-                for_block(multiply, step - 3)
+            if step + LEAD - 1 < PASSES:
+                for_half(deviation, step + LEAD - 1)
+            for r in range(ROW_TILES):
+                b, last = divmod(step - 3 - r, PASSES)
+                if last == PASSES - 1 and 0 <= b < BLOCKS - 1:
+                    multiply(b, r)
             if step - 6 < LAST_BLOCK:
                 for_block(add_bias, step - 6)
             if step - 1 >= LAST_BLOCK:

@@ -166,6 +166,9 @@ def tile_decoder_pb_e_kernel(tc, h7_pre, g7, be7, W8_words, W8_scales, b8, out):
         sums_bank = psum_sums.tile([P, 2, HALF * PACK], F32, name="sums")
         pending = []
 
+        def by_matmul(group):
+            return group % PASSES == PASSES - 1 and 3 * PASSES <= group < LAST_BLOCK
+
         def transpose(group):
             b, g = divmod(group, PASSES)
             half, place = divmod(group, HALF)
@@ -179,11 +182,12 @@ def tile_decoder_pb_e_kernel(tc, h7_pre, g7, be7, W8_words, W8_scales, b8, out):
             x_bank = psum_x.tile([P, PACK, ROWS], BF16, tag="x_bank")
             for t in range(PACK):
                 for r in range(ROW_TILES):
-                    nc.tensor.transpose(
-                        x_bank[:, t, r * P : (r + 1) * P],
-                        x_rows[(b, r)][:, K_PASS * g + t : K_PASS * (g + 1) : PACK],
-                        ident[:],
-                    )
+                    features = x_rows[(b, r)][:, K_PASS * g + t : K_PASS * (g + 1) : PACK]
+                    turned = x_bank[:, t, r * P : (r + 1) * P]
+                    if by_matmul(group):
+                        nc.tensor.matmul(out=turned, lhsT=features, rhs=ident[:], start=True, stop=True)
+                    else:
+                        nc.tensor.transpose(turned, features, ident[:])
                     run(pending[:3])
                     pending[:3] = []
             x_banks[group] = x_bank

from contextlib import ExitStack

import concourse.mybir as mybir
from concourse.masks import make_identity

F32 = mybir.dt.float32
BF16 = mybir.dt.bfloat16
I32 = mybir.dt.int32
U32 = mybir.dt.uint32
U8 = mybir.dt.uint8
FP8X4 = mybir.dt.float8_e4m3fn_x4
ALU = mybir.AluOpType
ACT = mybir.ActivationFunctionType

P = 128
BLOCKS = 8
ROWS = 256
ROW_TILES = ROWS // P
FEATURES = 2048
CHANNELS = 256
PACK = 4
K_PASS = P * PACK
PASSES = FEATURES // K_PASS
GROUPS = BLOCKS * PASSES
PAIR = 2
HALF = 2
EPS = 1e-5
WARM = 4
LEAD = 5

LAST_BLOCK = GROUPS - PASSES

FLOPS = 2 * BLOCKS * ROWS * FEATURES * CHANNELS


def tile_decoder_pb_e_kernel(tc, h7_pre, g7, be7, W8_words, W8_scales, b8, out):
    nc = tc.nc
    with ExitStack() as ctx:
        keep = ctx.enter_context(tc.tile_pool(name="keep", bufs=1))
        small = ctx.enter_context(tc.tile_pool(name="small", bufs=8))
        work = ctx.enter_context(tc.tile_pool(name="work", bufs=3))
        psum_x = ctx.enter_context(tc.psum_pool(name="psum_x", bufs=LEAD + 1))
        psum_sums = ctx.enter_context(tc.psum_pool(name="psum_sums", bufs=1))
        psum_out = ctx.enter_context(tc.psum_pool(name="psum_out", bufs=1))
        ctx.enter_context(tc.manual_schedule())

        wide = keep.tile([P, K_PASS], BF16)
        nc.vector.memset(wide[:], 0.0)
        gain_rows = keep.tile([P, K_PASS], BF16)
        nc.vector.memset(gain_rows[2 * GROUPS : P, :], 0.0)
        one = keep.tile([P, 1], F32)
        nc.vector.memset(one[:], 1.0)
        ones = keep.tile([P, 1], BF16)
        nc.vector.memset(ones[:], 1.0)
        w_planes = keep.tile([P, GROUPS, CHANNELS], U8, align_bytes=64)
        nc.vector.memset(w_planes[:].bitcast(I32), 0)
        ident_f32 = keep.tile([P, P], F32)
        make_identity(nc, ident_f32[:])
        ident = keep.tile([P, P], BF16)
        make_identity(nc, ident[:])

        x_rows = {}
        w_words = {}

        def load_x(b):
            for r in range(ROW_TILES):
                x_tile = keep.tile([P, FEATURES], BF16, name="x_%d_%d" % (b, r))
                x_rows[(b, r)] = x_tile
            width = K_PASS if b == 0 else HALF * K_PASS
            for first in range(0, FEATURES, width):
                cols = slice(first, first + width)
                for r in range(ROW_TILES):
                    nc.sync.dma_start(out=x_rows[(b, r)][:, cols], in_=h7_pre[b, r * P : (r + 1) * P, cols])

        def load_w(b):
            w_tile = keep.tile([P, PASSES, CHANNELS], U32, name="w_words_%d" % b, align_bytes=64)
            nc.sync.dma_start(
                out=w_tile[:].bitcast(I32),
                in_=W8_words[PASSES * b : PASSES * (b + 1)].rearrange("g p n t -> p g (n t)").bitcast(I32),
            )
            w_words[b] = w_tile

        nc.scalar.dma_start(out=gain_rows[0:GROUPS, :], in_=g7.rearrange("b (g k) -> (b g) k", g=PASSES))
        nc.scalar.dma_start(out=gain_rows[GROUPS : 2 * GROUPS, :], in_=be7.rearrange("b (g k) -> (b g) k", g=PASSES))
        warm = keep.tile([P, 1], F32)
        nc.scalar.activation(out=warm[:], in_=one[:], func=ACT.Abs_reciprocal_sqrt)

        for b in range(4):
            load_x(b)
        load_w(0)
        scale_rows = W8_scales.rearrange("g (q r) c -> r q g c", r=4)
        for r in range(4):
            nc.sync.dma_start(out=w_planes[r:P:32, :, :].bitcast(I32), in_=scale_rows[r].bitcast(I32))
        load_x(4)
        bias_all = keep.tile([P, BLOCKS, CHANNELS], BF16)
        nc.sync.dma_start(
            out=bias_all[:].rearrange("p b c -> p (b c)"),
            in_=b8.rearrange("b c -> (b c)").partition_broadcast(P),
        )
        for b in range(5, BLOCKS):
            load_w(b - 4)
            load_x(b)
        for b in range(BLOCKS - 4, BLOCKS):
            load_w(b)

        gain_cols = keep.tile([P, 2 * GROUPS, PAIR, PAIR], F32)

        def transpose_gains():
            gain_bank = psum_out.tile([P, PAIR, ROWS], F32, tag="product")
            for u in range(PAIR):
                nc.tensor.transpose(
                    gain_bank[:, u, 0:P], gain_rows[:].bitcast(F32)[:, u : K_PASS // PAIR : PAIR], ident_f32[:]
                )
            nc.vector.tensor_copy(
                out=gain_cols[:],
                in_=gain_bank[:, :, 0:P].bitcast(BF16).rearrange("p u (r e) -> p r u e", e=PAIR)[:, 0 : 2 * GROUPS],
            )

        warm_bank = psum_out.tile([P, K_PASS], F32, tag="product")
        for i in range(WARM):
            nc.tensor.matmul(out=warm_bank[:], lhsT=wide[:, 0:P], rhs=wide[:], start=True, stop=True)

        moments = {}
        x_banks = {}
        scale_of = {}
        rstd_of = {}
        shift_of = {}
        planes_of = {}
        quantised = {}
        products = {}
        logits_of = {}
        last_sums = {}

        def on_scalar(group):
            return group not in (0, HALF)

        def norm_on_scalar(group):
            return group == GROUPS - 3

        def sums_work(half, places):
            sums = sums_bank[:, half % 2]

            def one(place, t, r):
                b, g = divmod(HALF * half + place, PASSES)
                f = PACK * place + t
                nc.tensor.matmul(
                    out=sums[:, f : f + 1],
                    lhsT=x_rows[(b, r)][:, K_PASS * g + t : K_PASS * (g + 1) : PACK],
                    rhs=ones[:],
                    start=(r == 0),
                    stop=(r == ROW_TILES - 1),
                )

            return [
                (one, place, t, r)
                for place in places
                if on_scalar(HALF * half + place)
                for t in range(PACK)
                for r in range(ROW_TILES)
            ]

        def run(calls):
            for call in calls:
                call[0](call[1], call[2], call[3])

        sums_bank = psum_sums.tile([P, 2, HALF * PACK], F32, name="sums")
        pending = []

        def by_matmul(group):
            return group % PASSES == PASSES - 1 and 3 * PASSES <= group < LAST_BLOCK

        def transpose(group):
            b, g = divmod(group, PASSES)
            half, place = divmod(group, HALF)
            if place == 0:
                moments_tile = small.tile([P, HALF * PAIR * 6], F32, name="moments")
                moments[half] = moments_tile
            if half < 2:
                run(sums_work(half, [place]))
            if 1 <= half < GROUPS // HALF - 1 and place == (1 if half == 1 else 0):
                pending.extend(sums_work(half + 1, range(HALF)))
            x_bank = psum_x.tile([P, PACK, ROWS], BF16, tag="x_bank")
            for t in range(PACK):
                for r in range(ROW_TILES):
                    features = x_rows[(b, r)][:, K_PASS * g + t : K_PASS * (g + 1) : PACK]
                    turned = x_bank[:, t, r * P : (r + 1) * P]
                    if by_matmul(group):
                        nc.tensor.matmul(out=turned, lhsT=features, rhs=ident[:], start=True, stop=True)
                    else:
                        nc.tensor.transpose(turned, features, ident[:])
                    run(pending[:3])
                    pending[:3] = []
            x_banks[group] = x_bank

        def statistics(group):
            if on_scalar(group):
                return
            half, place = divmod(group, HALF)
            for u in range(PAIR):
                at = 6 * (PAIR * place + u)
                nc.vector.bn_stats(out=moments[half][:, at : at + 6], in_=x_banks[group][:, PAIR * u : PAIR * (u + 1), :].rearrange("p e n -> p n e"))

        def means(group):
            half, place = divmod(group, HALF)
            if not on_scalar(group) or (place == 1 and on_scalar(group - 1)):
                return
            first = place
            last = HALF if on_scalar(HALF * half + 1) else 1
            columns = slice(PACK * first, PACK * last)
            triples = moments[half][:].rearrange("p (f s) -> p f s", s=3)
            nc.scalar.activation(
                out=triples[:, columns, 1],
                in_=sums_bank[:, half % 2, columns],
                func=ACT.Copy,
                scale=1.0 / ROWS,
            )

        def squared_deviations(group):
            if not on_scalar(group):
                return
            half, place = divmod(group, HALF)
            triples = moments[half][:].rearrange("p (f s) -> p f s", s=3)
            for t in range(PACK):
                f = PACK * place + t
                squares = work.tile([P, ROWS], BF16)
                nc.scalar.activation(
                    out=squares[:],
                    in_=x_banks[group][:, t, :],
                    func=ACT.Square,
                    bias=triples[:, f : f + 1, 1],
                    scale=-1.0,
                    accum_out=triples[:, f : f + 1, 2],
                )

        def deviation(half):
            triples = moments[half][:].rearrange("p (f s) -> p f s", s=3)
            rstd = small.tile([P, HALF * PACK], F32)
            nc.scalar.activation(
                out=rstd[:], in_=triples[:, :, 2], func=ACT.Abs_reciprocal_sqrt, bias=EPS, scale=1.0 / ROWS
            )
            rstd_of[half] = rstd

        def scale_and_shift(half):
            triples = moments[half][:].rearrange("p (f s) -> p f s", s=3)
            rstd = rstd_of[half]
            engine = nc.vector if half == 0 else nc.gpsimd
            gain = gain_cols[:, HALF * half : HALF * (half + 1)].rearrange("p r u e -> p (r u e)")
            scale = small.tile([P, HALF * PACK], F32)
            engine.tensor_tensor(out=scale[:], in0=rstd[:], in1=gain, op=ALU.mult)
            scale_of[half] = scale
            mean_scaled = small.tile([P, HALF * PACK], F32)
            engine.tensor_tensor(out=mean_scaled[:], in0=triples[:, :, 1], in1=scale[:], op=ALU.mult)
            beta = gain_cols[:, GROUPS + HALF * half : GROUPS + HALF * (half + 1)].rearrange("p r u e -> p (r u e)")
            shift = small.tile([P, HALF * PACK], F32)
            engine.tensor_tensor(out=shift[:], in0=beta, in1=mean_scaled[:], op=ALU.subtract)
            shift_of[half] = shift

        def scalar_planes(group):
            return 1 if group % PASSES == PASSES - 1 and PASSES <= group < LAST_BLOCK else 0

        def planes_tile(group):
            if group not in planes_of:
                planes = work.tile([P, PACK, ROWS], BF16, bufs=7)
                planes_of[group] = planes
            return planes_of[group]

        def normalise_on_scalar(group, t):
            half, place = divmod(group, HALF)
            f = PACK * place + t
            nc.scalar.activation(
                out=planes_tile(group)[:, t, :],
                in_=x_banks[group][:, t, :],
                func=ACT.Identity,
                bias=shift_of[half][:, f : f + 1],
                scale=scale_of[half][:, f : f + 1],
            )

        def help_normalise(group):
            for t in range(scalar_planes(group)):
                normalise_on_scalar(group, t)

        def normalise(group):
            half, place = divmod(group, HALF)
            scale, shift = scale_of[half], shift_of[half]
            planes = planes_tile(group)
            for t in range(scalar_planes(group), PACK):
                f = PACK * place + t
                if norm_on_scalar(group):
                    normalise_on_scalar(group, t)
                else:
                    nc.vector.tensor_scalar(
                        out=planes[:, t, :],
                        in0=x_banks[group][:, t, :],
                        scalar1=scale[:, f : f + 1],
                        scalar2=shift[:, f : f + 1],
                        op0=ALU.mult,
                        op1=ALU.add,
                    )

        def regroup(group):
            b, g = divmod(group, PASSES)
            if g == 0:
                grouped = work.tile([P, PASSES, ROWS, PACK], BF16, align_bytes=64)
                a_codes = work.tile([P, PASSES, ROWS], U32, align_bytes=64)
                a_planes = work.tile([P, PASSES, ROWS], U8, align_bytes=64)
                quantised[b] = (grouped, a_codes, a_planes)
            side_by_side = quantised[b][0][:, g].rearrange("p (c i) t -> p c t i", i=4)
            by_feature = planes_of[group][:].rearrange("p t (c i) -> p c t i", i=4)
            nc.vector.tensor_scalar_max(side_by_side, by_feature, 0.0)

        def quantise(group):
            b, g = divmod(group, PASSES)
            grouped, a_codes, a_planes = quantised[b]
            nc.vector.quantize_mx(
                out=a_codes[:, g, :].bitcast(FP8X4),
                scales=a_planes[:, g, :],
                in_=grouped[:, g].rearrange("p n t -> p (n t)"),
            )

        def multiply(b, r):
            grouped, a_codes, a_planes = quantised[b]
            if r == 0:
                product = psum_out.tile([P, ROW_TILES, CHANNELS], F32, tag="product")
                products[b] = product
            rows = slice(r * P, (r + 1) * P)
            for g in range(PASSES):
                nc.tensor.matmul_mx(
                    out=products[b][:, r, :],
                    lhsT=a_codes[:, g, rows].bitcast(FP8X4),
                    lhsT_scale=a_planes[:, g, rows],
                    rhs=w_words[b][:, g, :].bitcast(FP8X4),
                    rhs_scale=w_planes[:, PASSES * b + g, :],
                    start=(g == 0),
                    stop=(g == PASSES - 1),
                )

        def multiply_last(group):
            b, g = divmod(group, PASSES)
            grouped, a_codes, a_planes = quantised[b]
            for r in range(ROW_TILES):
                if g == 0:
                    last_acc = psum_x.tile([P, CHANNELS], F32, tag="x_bank")
                    last_sums[r] = last_acc
                rows = slice(r * P, (r + 1) * P)
                nc.tensor.matmul_mx(
                    out=last_sums[r][:],
                    lhsT=a_codes[:, g, rows].bitcast(FP8X4),
                    lhsT_scale=a_planes[:, g, rows],
                    rhs=w_words[b][:, g, :].bitcast(FP8X4),
                    rhs_scale=w_planes[:, group, :],
                    start=(g == 0),
                    stop=(g == PASSES - 1),
                )

        def finish_last():
            for r in range(ROW_TILES):
                last_logits = work.tile([P, CHANNELS], F32, bufs=ROW_TILES)
                nc.vector.tensor_tensor(
                    out=last_logits[:], in0=last_sums[r][:], in1=bias_all[:, BLOCKS - 1, :], op=ALU.add
                )
                last_probs = work.tile([P, CHANNELS], F32, bufs=ROW_TILES)
                nc.scalar.activation(out=last_probs[:], in_=last_logits[:], func=ACT.Sigmoid)
                nc.sync.dma_start(out=out[r * P : (r + 1) * P, BLOCKS - 1, :], in_=last_probs[:])

        def add_bias(b):
            logits = work.tile([P, ROW_TILES, CHANNELS], F32, bufs=BLOCKS)
            nc.vector.tensor_tensor(
                out=logits[:],
                in0=products[b][:],
                in1=bias_all[:, b, :].unsqueeze(1).to_broadcast([P, ROW_TILES, CHANNELS]),
                op=ALU.add,
            )
            logits_of[b] = logits

        def squash_and_store(b):
            probs = work.tile([P, ROW_TILES, CHANNELS], F32, bufs=BLOCKS)
            nc.scalar.activation(out=probs[:], in_=logits_of[b][:], func=ACT.Sigmoid)
            nc.sync.dma_start(out=out.rearrange("(r n) b c -> n r b c", r=ROW_TILES)[:, :, b, :], in_=probs[:])

        def for_group(stage, group):
            if 0 <= group < GROUPS:
                stage(group)

        def for_half(stage, last_group):
            if 0 <= last_group < GROUPS and last_group % HALF == HALF - 1:
                stage(last_group // HALF)

        def for_block(stage, last_group):
            if 0 <= last_group < GROUPS and last_group % PASSES == PASSES - 1:
                stage(last_group // PASSES)

        for step in range(-LEAD, GROUPS + 7):
            for_group(means, step + LEAD - 1)
            if step + LEAD - 2 >= PASSES:
                for_half(deviation, step + LEAD - 2)
            for_half(scale_and_shift, step + LEAD - 2)
            if step - 2 < LAST_BLOCK:
                for_group(quantise, step - 2)
            for_group(regroup, step - 1)
            for_group(transpose, step + LEAD)
            for_group(normalise, step)
            for_group(help_normalise, step + 1)
            for_group(squared_deviations, step + LEAD - 1)
            if step + LEAD - 1 < PASSES:
                for_half(deviation, step + LEAD - 1)
            for r in range(ROW_TILES):
                b, last = divmod(step - 3 - r, PASSES)
                if last == PASSES - 1 and 0 <= b < BLOCKS - 1:
                    multiply(b, r)
            if step - 6 < LAST_BLOCK:
                for_block(add_bias, step - 6)
            if step - 1 >= LAST_BLOCK:
                for_group(quantise, step - 1)
                for_group(multiply_last, step - 1)
            for_group(statistics, step + LEAD)
            if step + LEAD == HALF - 1:
                transpose_gains()
            for b in range(BLOCKS - 1):
                if step == max(PASSES * b + PASSES - 1 + 7, GROUPS - LEAD + 2 + b):
                    squash_and_store(b)
        finish_last()
